import numpy as np
import ml_dtypes


def mxq(x, axis, fmt="e4m3"):
    dtype, down = {"e4m3": (ml_dtypes.float8_e4m3fn, 7), "e5m2": (ml_dtypes.float8_e5m2, 14)}[fmt]
    v = np.moveaxis(np.asarray(x, np.float32).astype(ml_dtypes.bfloat16).astype(np.float64), axis, -1)
    blocks = v.reshape(v.shape[:-1] + (-1, 32))
    amax = np.abs(blocks).max(-1, keepdims=True)
    byte = np.maximum(np.where(amax > 0, np.frexp(amax)[1] - 1 + 127, 0) - down, 1)
    scale = np.exp2(byte - 127.0)
    codes = (blocks / scale).astype(np.float32).astype(dtype).astype(np.float64)
    return np.moveaxis((codes * scale).reshape(v.shape), -1, axis)


WIDE = False


def mx_kscale(k):
    if not WIDE:
        return np.ones(k)
    levels = np.array([10, -10, 5, -5, 0])
    a = np.random.permutation(np.resize(levels, k // 512 * 4)).reshape(k // 512, 4)
    idx = np.arange(k)
    return np.exp2(a[idx // 512, idx % 128 // 32])


BF16 = ml_dtypes.bfloat16


def bf(x):
    return np.asarray(x, np.float32).astype(BF16)


def f64(x):
    return np.asarray(x).astype(np.float64)


B, P, STATE, PRE, LAT, OUT = 1024, 4, 12, 512, 512, 32
N = B * P
F = LAT + LAT


def prelu(v, a):
    return np.where(v >= 0, v, a * v)


def setup_inputs():
    s, u = mx_kscale(PRE), mx_kscale(PRE)
    return {
        "pre_child": bf(np.random.standard_normal((N, PRE)) * s),
        "pre_parent": bf(np.random.standard_normal((N, PRE)) * u),
        "ac": bf(0.25 + 0.05 * np.random.standard_normal(1)),
        "Wc2": bf(np.random.standard_normal((PRE, LAT)) / np.sqrt(PRE) / s[:, None]),
        "bc2": bf(np.random.standard_normal(LAT) * 0.2),
        "ap": bf(0.25 + 0.05 * np.random.standard_normal(1)),
        "Wp2": bf(np.random.standard_normal((PRE, LAT)) / np.sqrt(PRE) / u[:, None]),
        "bp2": bf(np.random.standard_normal(LAT) * 0.2),
        "Wl1": bf(np.random.standard_normal((F, PRE)) * 1.5 / np.sqrt(F)),
        "bl1": bf(np.random.standard_normal(PRE) * 0.2),
    }


def reference(pre_child, pre_parent, ac, Wc2, bc2, ap, Wp2, bp2, Wl1, bl1):
    hc = prelu(f64(pre_child), f64(ac))
    hp = prelu(f64(pre_parent), f64(ap))
    ch = np.tanh((mxq(hc, 1, "e4m3") @ mxq(f64(Wc2), 0, "e4m3")) + f64(bc2))
    pa = np.tanh((mxq(hp, 1, "e4m3") @ mxq(f64(Wp2), 0, "e4m3")) + f64(bp2))
    z = np.concatenate([ch, pa], axis=-1)
    return np.tanh((mxq(z, 1, "e4m3") @ mxq(f64(Wl1), 0, "e4m3")) + f64(bl1))

@@ -1,0 +1,257 @@
+from contextlib import ExitStack
+
+import concourse.mybir as mybir
+from concourse.masks import make_identity
+
+F32 = mybir.dt.float32
+BF16 = mybir.dt.bfloat16
+U32 = mybir.dt.uint32
+U8 = mybir.dt.uint8
+FP8X4 = mybir.dt.float8_e4m3fn_x4
+ALU = mybir.AluOpType
+ACT = mybir.ActivationFunctionType
+
+P = 128
+PACK = 4
+K_PASS = P * PACK
+ROWS = 4096
+WIDTH = 512
+BLOCK = 512
+ROW_TILES = BLOCK // P
+N_BLOCKS = ROWS // BLOCK
+N_UNITS = 2 * N_BLOCKS
+
+SCALAR_COLS = 192
+VECTOR_COLS = BLOCK - SCALAR_COLS
+
+FLOPS = 2 * ROWS * WIDTH * WIDTH * 2 + 2 * ROWS * (2 * WIDTH) * WIDTH
+
+
+def tile_rvnn_pa_t_kernel(
+    tc, pre_child, pre_parent, ac, Wc2, bc2, ap, Wp2, bp2, Wl1, bl1, out
+):
+    nc = tc.nc
+    streams = (pre_child, pre_parent)
+
+    with ExitStack() as ctx:
+        const = ctx.enter_context(tc.tile_pool(name="const", bufs=1))
+        x_pool = ctx.enter_context(tc.tile_pool(name="x_pool", bufs=N_UNITS))
+        work = ctx.enter_context(tc.tile_pool(name="work", bufs=3))
+        out_pool = ctx.enter_context(tc.tile_pool(name="out_pool", bufs=3))
+        ps_x = ctx.enter_context(tc.psum_pool(name="ps_x", bufs=2))
+        ps_1 = ctx.enter_context(tc.psum_pool(name="ps_1", bufs=4))
+        ps_2 = ctx.enter_context(tc.psum_pool(name="ps_2", bufs=2))
+
+        def load_x(u):
+            b, s = divmod(u, 2)
+            x = x_pool.tile([P, ROW_TILES, WIDTH], BF16, tag="x", name="x%d" % u)
+            rows = streams[s][b * BLOCK : (b + 1) * BLOCK, :]
+            nc.sync.dma_start(out=x[:], in_=rows.rearrange("(p a) k -> p a k", a=ROW_TILES))
+            return x
+
+        def load_first_weight(w, name):
+            raw = const.tile([P, PACK, WIDTH], BF16, name=name)
+            nc.sync.dma_start(
+                out=raw[:].rearrange("p (h e) c -> p h e c", e=2),
+                in_=w.rearrange("(h p e) c -> p h e c", h=2, e=2),
+            )
+            return raw
+
+        x_tiles = [load_x(0)]
+        w_raw = [load_first_weight(Wc2, "wc_raw")]
+        x_tiles.append(load_x(1))
+        w_raw.append(load_first_weight(Wp2, "wp_raw"))
+        x_tiles.append(load_x(2))
+        x_tiles.append(load_x(3))
+        wl_raw = const.tile([P, 2, PACK, WIDTH], BF16, name="wl_raw")
+        nc.sync.dma_start(out=wl_raw[:], in_=Wl1.rearrange("(g p j) c -> p g j c", g=2, j=PACK))
+        for u in range(4, N_UNITS):
+            x_tiles.append(load_x(u))
+
+        slopes = []
+        biases = []
+        with nc.allow_non_contiguous_dma(reason="a few small vectors, once"):
+            for s, (a_in, b_in) in enumerate(((ac, bc2), (ap, bp2))):
+                a_bf = const.tile([P, 1], BF16, name="a_bf%d" % s)
+                nc.scalar.dma_start(out=a_bf[:], in_=a_in.partition_broadcast(P))
+                b_bf = const.tile([P, PACK], BF16, name="b_bf%d" % s)
+                nc.scalar.dma_start(out=b_bf[:], in_=b_in.rearrange("(p t) -> p t", t=PACK))
+                a_f = const.tile([P, 1], F32, name="a_f%d" % s)
+                nc.vector.tensor_copy(out=a_f[:], in_=a_bf[:])
+                b_f = const.tile([P, PACK], F32, name="b_f%d" % s)
+                nc.vector.tensor_copy(out=b_f[:], in_=b_bf[:])
+                slopes.append(a_f)
+                biases.append(b_f)
+            bl_all = const.tile([P, WIDTH], BF16, name="bl_all")
+            nc.scalar.dma_start(out=bl_all[:], in_=bl1.partition_broadcast(P))
+
+        ident = const.tile([P, P], F32, name="ident")
+        make_identity(nc, ident[:])
+
+        warm = const.tile([P, 1], F32, name="warm")
+        nc.vector.memset(warm[:], 0.0)
+        nc.scalar.activation(out=warm[:], in_=warm[:], func=ACT.Tanh)
+
+        w_codes = {}
+        w_scales = {}
+
+        def prepare_weight(n):
+            grouped = work.tile([P, WIDTH, PACK], BF16, tag="w_grouped", align_bytes=64)
+            if n < 2:
+                nc.vector.tensor_copy(
+                    out=grouped[:].rearrange("p (t q) j -> p t q j", t=PACK),
+                    in_=w_raw[n][:].rearrange("p j (q t) -> p t q j", t=PACK),
+                )
+            else:
+                nc.vector.tensor_copy(
+                    out=grouped[:], in_=wl_raw[:, n - 2, :, :].rearrange("p j c -> p c j")
+                )
+            codes = const.tile([P, WIDTH], U32, name="w_codes%d" % n, align_bytes=64)
+            scales = const.tile([P, WIDTH], U8, name="w_scales%d" % n, align_bytes=64)
+            nc.vector.quantize_mx(
+                out=codes[:].bitcast(FP8X4),
+                scales=scales[:],
+                in_=grouped[:].rearrange("p c j -> p (c j)"),
+            )
+            w_codes[n] = codes
+            w_scales[n] = scales
+
+        def transpose_unit(u):
+            words = x_tiles[u][:].bitcast(F32)
+            banks = []
+            for half in range(2):
+                bank = ps_x.tile([P, 4, P], F32, tag="bank_x")
+                for a in range(2):
+                    for h in range(2):
+                        nc.tensor.transpose(
+                            bank[:, 2 * a + h, :],
+                            words[:, 2 * half + a, h * P : (h + 1) * P],
+                            ident[:],
+                        )
+                banks.append(bank)
+            return banks
+
+        def copy_out(banks):
+            xt = work.tile([P, BLOCK * PACK], BF16, tag="xt", align_bytes=64)
+            xt_words = xt[:].bitcast(F32).rearrange("p (a r h) -> p a r h", a=ROW_TILES, h=2)
+            for half in range(2):
+                nc.scalar.copy(
+                    out=xt_words[:, 2 * half : 2 * half + 2, :, :],
+                    in_=banks[half][:].rearrange("p (a h) r -> p a r h", h=2),
+                )
+            return xt
+
+        def prelu(u, xt):
+            pos = work.tile([P, BLOCK * PACK], BF16, tag="pos", align_bytes=64)
+            neg = work.tile([P, BLOCK * PACK], BF16, tag="neg", align_bytes=64)
+            nc.vector.tensor_scalar(
+                out=pos[:], in0=xt[:], scalar1=0.0, scalar2=None, op0=ALU.max
+            )
+            nc.vector.tensor_scalar(
+                out=neg[:], in0=xt[:], scalar1=0.0, scalar2=slopes[u % 2][:, 0:1],
+                op0=ALU.min, op1=ALU.mult,
+            )
+            nc.vector.tensor_tensor(out=pos[:], in0=pos[:], in1=neg[:], op=ALU.add)
+            return pos
+
+        def quantise(values, tag):
+            codes = work.tile([P, BLOCK], U32, tag=tag + "_codes", bufs=6, align_bytes=64)
+            scales = work.tile([P, BLOCK], U8, tag=tag + "_scales", bufs=6, align_bytes=64)
+            nc.vector.quantize_mx(out=codes[:].bitcast(FP8X4), scales=scales[:], in_=values)
+            return codes, scales
+
+        def first_layer(u, h):
+            s = u % 2
+            planes = work.tile([P, PACK, BLOCK], BF16, tag="planes")
+            for t in range(PACK):
+                acc = ps_1.tile([P, BLOCK], F32, tag="acc_1")
+                cols = slice(t * P, (t + 1) * P)
+                nc.tensor.matmul_mx(
+                    out=acc[:],
+                    lhsT=w_codes[s][:, cols].bitcast(FP8X4),
+                    lhsT_scale=w_scales[s][:, cols],
+                    rhs=h[0][:].bitcast(FP8X4),
+                    rhs_scale=h[1][:],
+                    start=True,
+                    stop=True,
+                )
+                nc.scalar.activation(
+                    out=planes[:, t, :], in_=acc[:], func=ACT.Tanh,
+                    bias=biases[s][:, t : t + 1], scale=1.0,
+                )
+            return planes
+
+        def regroup(planes):
+            grouped = work.tile([P, BLOCK, PACK], BF16, tag="z_grouped", align_bytes=64)
+            nc.vector.tensor_copy(
+                out=grouped[:, :VECTOR_COLS, :].rearrange("p (c i) t -> p c t i", i=4),
+                in_=planes[:, :, :VECTOR_COLS].rearrange("p t (c i) -> p c t i", i=4),
+            )
+            nc.scalar.copy(
+                out=grouped[:, VECTOR_COLS:, :].rearrange("p (c i) t -> p c t i", i=4),
+                in_=planes[:, :, VECTOR_COLS:].rearrange("p t (c i) -> p c t i", i=4),
+            )
+            return grouped
+
+        def second_layer(b, row_tiles, z, result):
+            rows = out[b * BLOCK : (b + 1) * BLOCK, :].rearrange("(p a) c -> p a c", a=ROW_TILES)
+            for a in row_tiles:
+                acc = ps_2.tile([P, WIDTH], F32, tag="acc_2")
+                cols = slice(a * P, (a + 1) * P)
+                for g in range(2):
+                    nc.tensor.matmul_mx(
+                        out=acc[:],
+                        lhsT=z[g][0][:, cols].bitcast(FP8X4),
+                        lhsT_scale=z[g][1][:, cols],
+                        rhs=w_codes[2 + g][:].bitcast(FP8X4),
+                        rhs_scale=w_scales[2 + g][:],
+                        start=(g == 0),
+                        stop=(g == 1),
+                    )
+                nc.vector.tensor_tensor(
+                    out=result[:, a, :], in0=acc[:], in1=bl_all[:], op=ALU.add
+                )
+                nc.scalar.activation(out=result[:, a, :], in_=result[:, a, :], func=ACT.Tanh)
+                nc.sync.dma_start(out=rows[:, a, :], in_=result[:, a, :])
+
+        def is_unit(u):
+            return 0 <= u < N_UNITS
+
+        banks_of = {}
+        xt_of = {}
+        h_of = {}
+        hq_of = {}
+        planes_of = {}
+        grouped_of = {}
+        z_of = {}
+        result_of = {}
+        with tc.manual_schedule():
+            banks_of[0] = transpose_unit(0)
+            for i in range(N_UNITS + 5):
+                if is_unit(i):
+                    xt_of[i] = copy_out(banks_of[i])
+                if is_unit(i - 2):
+                    planes_of[i - 2] = first_layer(i - 2, hq_of[i - 2])
+                if is_unit(i - 1):
+                    h_of[i - 1] = prelu(i - 1, xt_of[i - 1])
+                if is_unit(i - 3):
+                    grouped_of[i - 3] = regroup(planes_of[i - 3])
+                if is_unit(i - 5):
+                    b, half = divmod(i - 5, 2)
+                    if half == 0:
+                        result_of[b] = out_pool.tile(
+                            [P, ROW_TILES, WIDTH], F32, tag="result", name="result%d" % b
+                        )
+                    second_layer(
+                        b, (2 * half, 2 * half + 1), (z_of[2 * b], z_of[2 * b + 1]), result_of[b]
+                    )
+                if is_unit(i + 1):
+                    banks_of[i + 1] = transpose_unit(i + 1)
+                if is_unit(i - 1):
+                    hq_of[i - 1] = quantise(h_of[i - 1][:], "h")
+                if is_unit(i - 3):
+                    z_of[i - 3] = quantise(
+                        grouped_of[i - 3][:].rearrange("p c t -> p (c t)"), "z"
+                    )
+                if i < 4:
+                    prepare_weight(i)

@@ -37,10 +37,9 @@ def tile_rvnn_pa_t_kernel(
         const = ctx.enter_context(tc.tile_pool(name="const", bufs=1))
         x_pool = ctx.enter_context(tc.tile_pool(name="x_pool", bufs=N_UNITS))
         work = ctx.enter_context(tc.tile_pool(name="work", bufs=3))
-        out_pool = ctx.enter_context(tc.tile_pool(name="out_pool", bufs=3))
-        ps_x = ctx.enter_context(tc.psum_pool(name="ps_x", bufs=2))
-        ps_1 = ctx.enter_context(tc.psum_pool(name="ps_1", bufs=4))
-        ps_2 = ctx.enter_context(tc.psum_pool(name="ps_2", bufs=2))
+        codes_pool = ctx.enter_context(tc.tile_pool(name="codes_pool", bufs=8))
+        out_pool = ctx.enter_context(tc.tile_pool(name="out_pool", bufs=8))
+        psum = ctx.enter_context(tc.psum_pool(name="psum", bufs=8))
 
         def load_x(u):
             b, s = divmod(u, 2)
@@ -58,9 +57,9 @@ def tile_rvnn_pa_t_kernel(
             return raw
 
         x_tiles = [load_x(0)]
-        w_raw = [load_first_weight(Wc2, "wc_raw")]
+        wc_raw = load_first_weight(Wc2, "wc_raw")
         x_tiles.append(load_x(1))
-        w_raw.append(load_first_weight(Wp2, "wp_raw"))
+        wp_raw = load_first_weight(Wp2, "wp_raw")
         x_tiles.append(load_x(2))
         x_tiles.append(load_x(3))
         wl_raw = const.tile([P, 2, PACK, WIDTH], BF16, name="wl_raw")
@@ -92,35 +91,28 @@ def tile_rvnn_pa_t_kernel(
         nc.vector.memset(warm[:], 0.0)
         nc.scalar.activation(out=warm[:], in_=warm[:], func=ACT.Tanh)
 
-        w_codes = {}
-        w_scales = {}
-
-        def prepare_weight(n):
-            grouped = work.tile([P, WIDTH, PACK], BF16, tag="w_grouped", align_bytes=64)
+        def regroup_weight(n, copy):
+            grouped = const.tile([P, WIDTH, PACK], BF16, name="w_grouped%d" % n, align_bytes=64)
             if n < 2:
-                nc.vector.tensor_copy(
+                copy(
                     out=grouped[:].rearrange("p (t q) j -> p t q j", t=PACK),
-                    in_=w_raw[n][:].rearrange("p j (q t) -> p t q j", t=PACK),
+                    in_=(wc_raw, wp_raw)[n][:].rearrange("p j (q t) -> p t q j", t=PACK),
                 )
             else:
-                nc.vector.tensor_copy(
-                    out=grouped[:], in_=wl_raw[:, n - 2, :, :].rearrange("p j c -> p c j")
-                )
-            codes = const.tile([P, WIDTH], U32, name="w_codes%d" % n, align_bytes=64)
-            scales = const.tile([P, WIDTH], U8, name="w_scales%d" % n, align_bytes=64)
-            nc.vector.quantize_mx(
-                out=codes[:].bitcast(FP8X4),
-                scales=scales[:],
-                in_=grouped[:].rearrange("p c j -> p (c j)"),
-            )
-            w_codes[n] = codes
-            w_scales[n] = scales
+                copy(out=grouped[:], in_=wl_raw[:, n - 2, :, :].rearrange("p j c -> p c j"))
+            return grouped
+
+        def quantise(values, tag):
+            codes = codes_pool.tile([P, BLOCK], U32, tag=tag + "_codes", align_bytes=64)
+            scales = codes_pool.tile([P, BLOCK], U8, tag=tag + "_scales", align_bytes=64)
+            nc.vector.quantize_mx(out=codes[:].bitcast(FP8X4), scales=scales[:], in_=values)
+            return codes, scales
 
         def transpose_unit(u):
             words = x_tiles[u][:].bitcast(F32)
             banks = []
             for half in range(2):
-                bank = ps_x.tile([P, 4, P], F32, tag="bank_x")
+                bank = psum.tile([P, 4, P], F32, tag="bank")
                 for a in range(2):
                     for h in range(2):
                         nc.tensor.transpose(
@@ -141,7 +133,7 @@ def tile_rvnn_pa_t_kernel(
                 )
             return xt
 
-        def prelu(u, xt):
+        def prelu_parts(u, xt):
             pos = work.tile([P, BLOCK * PACK], BF16, tag="pos", align_bytes=64)
             neg = work.tile([P, BLOCK * PACK], BF16, tag="neg", align_bytes=64)
             nc.vector.tensor_scalar(
@@ -151,25 +143,22 @@ def tile_rvnn_pa_t_kernel(
                 out=neg[:], in0=xt[:], scalar1=0.0, scalar2=slopes[u % 2][:, 0:1],
                 op0=ALU.min, op1=ALU.mult,
             )
+            return pos, neg
+
+        def prelu_join(pos, neg):
             nc.vector.tensor_tensor(out=pos[:], in0=pos[:], in1=neg[:], op=ALU.add)
             return pos
-
-        def quantise(values, tag):
-            codes = work.tile([P, BLOCK], U32, tag=tag + "_codes", bufs=6, align_bytes=64)
-            scales = work.tile([P, BLOCK], U8, tag=tag + "_scales", bufs=6, align_bytes=64)
-            nc.vector.quantize_mx(out=codes[:].bitcast(FP8X4), scales=scales[:], in_=values)
-            return codes, scales
 
         def first_layer(u, h):
             s = u % 2
             planes = work.tile([P, PACK, BLOCK], BF16, tag="planes")
             for t in range(PACK):
-                acc = ps_1.tile([P, BLOCK], F32, tag="acc_1")
+                acc = psum.tile([P, BLOCK], F32, tag="bank")
                 cols = slice(t * P, (t + 1) * P)
                 nc.tensor.matmul_mx(
                     out=acc[:],
-                    lhsT=w_codes[s][:, cols].bitcast(FP8X4),
-                    lhsT_scale=w_scales[s][:, cols],
+                    lhsT=w_q[s][0][:, cols].bitcast(FP8X4),
+                    lhsT_scale=w_q[s][1][:, cols],
                     rhs=h[0][:].bitcast(FP8X4),
                     rhs_scale=h[1][:],
                     start=True,
@@ -181,77 +170,100 @@ def tile_rvnn_pa_t_kernel(
                 )
             return planes
 
-        def regroup(planes):
-            grouped = work.tile([P, BLOCK, PACK], BF16, tag="z_grouped", align_bytes=64)
-            nc.vector.tensor_copy(
-                out=grouped[:, :VECTOR_COLS, :].rearrange("p (c i) t -> p c t i", i=4),
-                in_=planes[:, :, :VECTOR_COLS].rearrange("p t (c i) -> p c t i", i=4),
+        def regroup(copy, grouped, planes, cols):
+            copy(
+                out=grouped[:, cols, :].rearrange("p (c i) t -> p c t i", i=4),
+                in_=planes[:, :, cols].rearrange("p t (c i) -> p c t i", i=4),
             )
-            nc.scalar.copy(
-                out=grouped[:, VECTOR_COLS:, :].rearrange("p (c i) t -> p c t i", i=4),
-                in_=planes[:, :, VECTOR_COLS:].rearrange("p t (c i) -> p c t i", i=4),
-            )
-            return grouped
 
-        def second_layer(b, row_tiles, z, result):
-            rows = out[b * BLOCK : (b + 1) * BLOCK, :].rearrange("(p a) c -> p a c", a=ROW_TILES)
-            for a in row_tiles:
-                acc = ps_2.tile([P, WIDTH], F32, tag="acc_2")
+        def second_layer_matmuls(n):
+            b, half = divmod(n, 2)
+            accs = []
+            for a in (2 * half, 2 * half + 1):
+                acc = psum.tile([P, WIDTH], F32, tag="bank")
                 cols = slice(a * P, (a + 1) * P)
                 for g in range(2):
                     nc.tensor.matmul_mx(
                         out=acc[:],
-                        lhsT=z[g][0][:, cols].bitcast(FP8X4),
-                        lhsT_scale=z[g][1][:, cols],
-                        rhs=w_codes[2 + g][:].bitcast(FP8X4),
-                        rhs_scale=w_scales[2 + g][:],
+                        lhsT=z_q[2 * b + g][0][:, cols].bitcast(FP8X4),
+                        lhsT_scale=z_q[2 * b + g][1][:, cols],
+                        rhs=w_q[2 + g][0][:].bitcast(FP8X4),
+                        rhs_scale=w_q[2 + g][1][:],
                         start=(g == 0),
                         stop=(g == 1),
                     )
-                nc.vector.tensor_tensor(
-                    out=result[:, a, :], in0=acc[:], in1=bl_all[:], op=ALU.add
-                )
-                nc.scalar.activation(out=result[:, a, :], in_=result[:, a, :], func=ACT.Tanh)
-                nc.sync.dma_start(out=rows[:, a, :], in_=result[:, a, :])
+                accs.append(acc)
+            return accs
+
+        def add_bias(accs):
+            sums = []
+            for acc in accs:
+                total = out_pool.tile([P, WIDTH], F32, tag="total")
+                nc.vector.tensor_tensor(out=total[:], in0=acc[:], in1=bl_all[:], op=ALU.add)
+                sums.append(total)
+            return sums
+
+        def finish(n, sums):
+            b, half = divmod(n, 2)
+            rows = out[b * BLOCK : (b + 1) * BLOCK, :].rearrange("(p a) c -> p a c", a=ROW_TILES)
+            for k in range(2):
+                nc.scalar.activation(out=sums[k][:], in_=sums[k][:], func=ACT.Tanh)
+                nc.sync.dma_start(out=rows[:, 2 * half + k, :], in_=sums[k][:])
 
         def is_unit(u):
             return 0 <= u < N_UNITS
 
         banks_of = {}
         xt_of = {}
-        h_of = {}
-        hq_of = {}
+        parts_of = {}
+        h_q = {}
         planes_of = {}
         grouped_of = {}
-        z_of = {}
-        result_of = {}
+        z_q = {}
+        accs_of = {}
+        sums_of = {}
+        w_grouped = {}
+        w_q = {}
         with tc.manual_schedule():
             banks_of[0] = transpose_unit(0)
-            for i in range(N_UNITS + 5):
+            for i in range(N_UNITS + 7):
+                if is_unit(i - 6):
+                    sums_of[i - 6] = add_bias(accs_of[i - 6])
+                if is_unit(i - 3):
+                    grouped_of[i - 3] = work.tile(
+                        [P, BLOCK, PACK], BF16, tag="z_grouped", name="z_grouped", align_bytes=64
+                    )
+                    regroup(
+                        nc.scalar.copy, grouped_of[i - 3], planes_of[i - 3],
+                        slice(VECTOR_COLS, BLOCK),
+                    )
                 if is_unit(i):
                     xt_of[i] = copy_out(banks_of[i])
                 if is_unit(i - 2):
-                    planes_of[i - 2] = first_layer(i - 2, hq_of[i - 2])
+                    planes_of[i - 2] = first_layer(i - 2, h_q[i - 2])
                 if is_unit(i - 1):
-                    h_of[i - 1] = prelu(i - 1, xt_of[i - 1])
+                    parts_of[i - 1] = prelu_parts(i - 1, xt_of[i - 1])
                 if is_unit(i - 3):
-                    grouped_of[i - 3] = regroup(planes_of[i - 3])
-                if is_unit(i - 5):
-                    b, half = divmod(i - 5, 2)
-                    if half == 0:
-                        result_of[b] = out_pool.tile(
-                            [P, ROW_TILES, WIDTH], F32, tag="result", name="result%d" % b
-                        )
-                    second_layer(
-                        b, (2 * half, 2 * half + 1), (z_of[2 * b], z_of[2 * b + 1]), result_of[b]
+                    regroup(
+                        nc.vector.tensor_copy, grouped_of[i - 3], planes_of[i - 3],
+                        slice(0, VECTOR_COLS),
                     )
+                if is_unit(i - 1):
+                    h = prelu_join(parts_of[i - 1][0], parts_of[i - 1][1])
                 if is_unit(i + 1):
                     banks_of[i + 1] = transpose_unit(i + 1)
-                if is_unit(i - 1):
-                    hq_of[i - 1] = quantise(h_of[i - 1][:], "h")
+                if is_unit(i - 5):
+                    accs_of[i - 5] = second_layer_matmuls(i - 5)
+                if is_unit(i - 6):
+                    finish(i - 6, sums_of[i - 6])
                 if is_unit(i - 3):
-                    z_of[i - 3] = quantise(
-                        grouped_of[i - 3][:].rearrange("p c t -> p (c t)"), "z"
-                    )
-                if i < 4:
-                    prepare_weight(i)
+                    z_q[i - 3] = quantise(grouped_of[i - 3][:].rearrange("p c t -> p (c t)"), "z")
+                if is_unit(i - 1):
+                    h_q[i - 1] = quantise(h[:], "h")
+                if i == 0:
+                    w_grouped[0] = regroup_weight(0, nc.vector.tensor_copy)
+                    w_q[0] = quantise(w_grouped[0][:].rearrange("p c j -> p (c j)"), "w")
+                if 1 <= i <= 3:
+                    w_grouped[i] = regroup_weight(i, nc.scalar.copy)
+                if 2 <= i <= 4:
+                    w_q[i - 1] = quantise(w_grouped[i - 1][:].rearrange("p c j -> p (c j)"), "w")

@@ -21,8 +21,9 @@ ROW_TILES = BLOCK // P
 N_BLOCKS = ROWS // BLOCK
 N_UNITS = 2 * N_BLOCKS
 
-SCALAR_COLS = 192
-VECTOR_COLS = BLOCK - SCALAR_COLS
+GPSIMD_COLS = 192
+SCALAR_COLS = 96
+VECTOR_COLS = BLOCK - SCALAR_COLS - GPSIMD_COLS
 
 FLOPS = 2 * ROWS * WIDTH * WIDTH * 2 + 2 * ROWS * (2 * WIDTH) * WIDTH
 
@@ -235,7 +236,14 @@ def tile_rvnn_pa_t_kernel(
                     )
                     regroup(
                         nc.scalar.copy, grouped_of[i - 3], planes_of[i - 3],
-                        slice(VECTOR_COLS, BLOCK),
+                        slice(VECTOR_COLS, VECTOR_COLS + SCALAR_COLS),
+                    )
+                    nc.gpsimd.tensor_scalar(
+                        out=grouped_of[i - 3][:, VECTOR_COLS + SCALAR_COLS :, :],
+                        in0=planes_of[i - 3][:, :, VECTOR_COLS + SCALAR_COLS :].rearrange(
+                            "p t c -> p c t"
+                        ),
+                        scalar1=1.0, scalar2=0.0, op0=ALU.mult, op1=ALU.add,
                     )
                 if is_unit(i):
                     xt_of[i] = copy_out(banks_of[i])

@@ -38,7 +38,7 @@ def tile_rvnn_pa_t_kernel(
         const = ctx.enter_context(tc.tile_pool(name="const", bufs=1))
         x_pool = ctx.enter_context(tc.tile_pool(name="x_pool", bufs=N_UNITS))
         work = ctx.enter_context(tc.tile_pool(name="work", bufs=3))
-        codes_pool = ctx.enter_context(tc.tile_pool(name="codes_pool", bufs=8))
+        codes_pool = ctx.enter_context(tc.tile_pool(name="codes_pool", bufs=4))
         out_pool = ctx.enter_context(tc.tile_pool(name="out_pool", bufs=8))
         psum = ctx.enter_context(tc.psum_pool(name="psum", bufs=8))
 
@@ -103,14 +103,14 @@ def tile_rvnn_pa_t_kernel(
                 copy(out=grouped[:], in_=wl_raw[:, n - 2, :, :].rearrange("p j c -> p c j"))
             return grouped
 
-        def quantise(values, tag):
-            codes = codes_pool.tile([P, BLOCK], U32, tag=tag + "_codes", align_bytes=64)
-            scales = codes_pool.tile([P, BLOCK], U8, tag=tag + "_scales", align_bytes=64)
+        def quantise(values, tag, bufs=4):
+            codes = codes_pool.tile([P, BLOCK], U32, tag=tag + "_codes", bufs=bufs, align_bytes=64)
+            scales = codes_pool.tile([P, BLOCK], U8, tag=tag + "_scales", bufs=bufs, align_bytes=64)
             nc.vector.quantize_mx(out=codes[:].bitcast(FP8X4), scales=scales[:], in_=values)
             return codes, scales
 
-        def transpose_unit(u):
-            words = x_tiles[u][:].bitcast(F32)
+        def transpose_unit(h):
+            words = h[:].bitcast(F32).rearrange("p (a w) -> p a w", a=ROW_TILES)
             banks = []
             for half in range(2):
                 bank = psum.tile([P, 4, P], F32, tag="bank")
@@ -125,23 +125,24 @@ def tile_rvnn_pa_t_kernel(
             return banks
 
         def copy_out(banks):
-            xt = work.tile([P, BLOCK * PACK], BF16, tag="xt", align_bytes=64)
-            xt_words = xt[:].bitcast(F32).rearrange("p (a r h) -> p a r h", a=ROW_TILES, h=2)
+            ht = work.tile([P, BLOCK * PACK], BF16, tag="ht", align_bytes=64)
+            ht_words = ht[:].bitcast(F32).rearrange("p (a r h) -> p a r h", a=ROW_TILES, h=2)
             for half in range(2):
                 nc.scalar.copy(
-                    out=xt_words[:, 2 * half : 2 * half + 2, :, :],
+                    out=ht_words[:, 2 * half : 2 * half + 2, :, :],
                     in_=banks[half][:].rearrange("p (a h) r -> p a r h", h=2),
                 )
-            return xt
+            return ht
 
-        def prelu_parts(u, xt):
+        def prelu_parts(u):
+            xt = x_tiles[u][:].rearrange("p a k -> p (a k)")
             pos = work.tile([P, BLOCK * PACK], BF16, tag="pos", align_bytes=64)
             neg = work.tile([P, BLOCK * PACK], BF16, tag="neg", align_bytes=64)
             nc.vector.tensor_scalar(
-                out=pos[:], in0=xt[:], scalar1=0.0, scalar2=None, op0=ALU.max
+                out=pos[:], in0=xt, scalar1=0.0, scalar2=None, op0=ALU.max
             )
             nc.vector.tensor_scalar(
-                out=neg[:], in0=xt[:], scalar1=0.0, scalar2=slopes[u % 2][:, 0:1],
+                out=neg[:], in0=xt, scalar1=0.0, scalar2=slopes[u % 2][:, 0:1],
                 op0=ALU.min, op1=ALU.mult,
             )
             return pos, neg
@@ -150,9 +151,9 @@ def tile_rvnn_pa_t_kernel(
             nc.vector.tensor_tensor(out=pos[:], in0=pos[:], in1=neg[:], op=ALU.add)
             return pos
 
-        def first_layer(u, h):
+        def first_layer_matmuls(u, h):
             s = u % 2
-            planes = work.tile([P, PACK, BLOCK], BF16, tag="planes")
+            accs = []
             for t in range(PACK):
                 acc = psum.tile([P, BLOCK], F32, tag="bank")
                 cols = slice(t * P, (t + 1) * P)
@@ -165,9 +166,15 @@ def tile_rvnn_pa_t_kernel(
                     start=True,
                     stop=True,
                 )
+                accs.append(acc)
+            return accs
+
+        def first_layer_tanh(u, accs):
+            planes = work.tile([P, PACK, BLOCK], BF16, tag="planes", bufs=4)
+            for t in range(PACK):
                 nc.scalar.activation(
-                    out=planes[:, t, :], in_=acc[:], func=ACT.Tanh,
-                    bias=biases[s][:, t : t + 1], scale=1.0,
+                    out=planes[:, t, :], in_=accs[t][:], func=ACT.Tanh,
+                    bias=biases[u % 2][:, t : t + 1], scale=1.0,
                 )
             return planes
 
@@ -214,64 +221,67 @@ def tile_rvnn_pa_t_kernel(
         def is_unit(u):
             return 0 <= u < N_UNITS
 
+        h_of = {}
         banks_of = {}
-        xt_of = {}
+        ht_of = {}
         parts_of = {}
         h_q = {}
+        accs1_of = {}
         planes_of = {}
         grouped_of = {}
         z_q = {}
-        accs_of = {}
+        accs2_of = {}
         sums_of = {}
         w_grouped = {}
         w_q = {}
         with tc.manual_schedule():
-            banks_of[0] = transpose_unit(0)
-            for i in range(N_UNITS + 7):
-                if is_unit(i - 6):
-                    sums_of[i - 6] = add_bias(accs_of[i - 6])
+            for i in range(N_UNITS + 11):
+                if is_unit(i - 9):
+                    sums_of[i - 9] = add_bias(accs2_of[i - 9])
                 if is_unit(i - 3):
-                    grouped_of[i - 3] = work.tile(
-                        [P, BLOCK, PACK], BF16, tag="z_grouped", name="z_grouped", align_bytes=64
-                    )
+                    accs1_of[i - 3] = first_layer_matmuls(i - 3, h_q[i - 3])
+                if is_unit(i - 5):
                     regroup(
-                        nc.scalar.copy, grouped_of[i - 3], planes_of[i - 3],
+                        nc.scalar.copy, grouped_of[i - 5], planes_of[i - 5],
                         slice(VECTOR_COLS, VECTOR_COLS + SCALAR_COLS),
                     )
+                if is_unit(i - 10):
+                    finish(i - 10, sums_of[i - 10])
+                if is_unit(i - 5):
                     nc.gpsimd.tensor_scalar(
-                        out=grouped_of[i - 3][:, VECTOR_COLS + SCALAR_COLS :, :],
-                        in0=planes_of[i - 3][:, :, VECTOR_COLS + SCALAR_COLS :].rearrange(
+                        out=grouped_of[i - 5][:, VECTOR_COLS + SCALAR_COLS :, :],
+                        in0=planes_of[i - 5][:, :, VECTOR_COLS + SCALAR_COLS :].rearrange(
                             "p t c -> p c t"
                         ),
                         scalar1=1.0, scalar2=0.0, op0=ALU.mult, op1=ALU.add,
                     )
-                if is_unit(i):
-                    xt_of[i] = copy_out(banks_of[i])
-                if is_unit(i - 2):
-                    planes_of[i - 2] = first_layer(i - 2, h_q[i - 2])
-                if is_unit(i - 1):
-                    parts_of[i - 1] = prelu_parts(i - 1, xt_of[i - 1])
                 if is_unit(i - 3):
+                    planes_of[i - 3] = first_layer_tanh(i - 3, accs1_of[i - 3])
+                if is_unit(i):
+                    parts_of[i] = prelu_parts(i)
+                if is_unit(i - 1):
+                    banks_of[i - 1] = transpose_unit(h_of[i - 1])
+                if is_unit(i - 8):
+                    accs2_of[i - 8] = second_layer_matmuls(i - 8)
+                if is_unit(i - 2):
+                    h_q[i - 2] = quantise(ht_of[i - 2][:], "h")
+                if is_unit(i - 1):
+                    ht_of[i - 1] = copy_out(banks_of[i - 1])
+                if is_unit(i):
+                    h_of[i] = prelu_join(parts_of[i][0], parts_of[i][1])
+                if is_unit(i - 4):
+                    grouped_of[i - 4] = work.tile(
+                        [P, BLOCK, PACK], BF16, tag="z_grouped", name="z_grouped", align_bytes=64
+                    )
                     regroup(
-                        nc.vector.tensor_copy, grouped_of[i - 3], planes_of[i - 3],
+                        nc.vector.tensor_copy, grouped_of[i - 4], planes_of[i - 4],
                         slice(0, VECTOR_COLS),
                     )
-                if is_unit(i - 1):
-                    h = prelu_join(parts_of[i - 1][0], parts_of[i - 1][1])
-                if is_unit(i + 1):
-                    banks_of[i + 1] = transpose_unit(i + 1)
                 if is_unit(i - 5):
-                    accs_of[i - 5] = second_layer_matmuls(i - 5)
-                if is_unit(i - 6):
-                    finish(i - 6, sums_of[i - 6])
-                if is_unit(i - 3):
-                    z_q[i - 3] = quantise(grouped_of[i - 3][:].rearrange("p c t -> p (c t)"), "z")
-                if is_unit(i - 1):
-                    h_q[i - 1] = quantise(h[:], "h")
-                if i == 0:
-                    w_grouped[0] = regroup_weight(0, nc.vector.tensor_copy)
-                    w_q[0] = quantise(w_grouped[0][:].rearrange("p c j -> p (c j)"), "w")
-                if 1 <= i <= 3:
+                    z_q[i - 5] = quantise(
+                        grouped_of[i - 5][:].rearrange("p c t -> p (c t)"), "z", bufs=8
+                    )
+                if i < 4:
                     w_grouped[i] = regroup_weight(i, nc.scalar.copy)
-                if 2 <= i <= 4:
+                if 1 <= i <= 4:
                     w_q[i - 1] = quantise(w_grouped[i - 1][:].rearrange("p c j -> p (c j)"), "w")

@@ -13,17 +13,12 @@ ACT = mybir.ActivationFunctionType
 
 P = 128
 PACK = 4
-K_PASS = P * PACK
 ROWS = 4096
 WIDTH = 512
 BLOCK = 512
 ROW_TILES = BLOCK // P
 N_BLOCKS = ROWS // BLOCK
 N_UNITS = 2 * N_BLOCKS
-
-GPSIMD_COLS = 192
-SCALAR_COLS = 96
-VECTOR_COLS = BLOCK - SCALAR_COLS - GPSIMD_COLS
 
 FLOPS = 2 * ROWS * WIDTH * WIDTH * 2 + 2 * ROWS * (2 * WIDTH) * WIDTH
 
@@ -39,8 +34,10 @@ def tile_rvnn_pa_t_kernel(
         x_pool = ctx.enter_context(tc.tile_pool(name="x_pool", bufs=N_UNITS))
         work = ctx.enter_context(tc.tile_pool(name="work", bufs=3))
         codes_pool = ctx.enter_context(tc.tile_pool(name="codes_pool", bufs=4))
-        out_pool = ctx.enter_context(tc.tile_pool(name="out_pool", bufs=8))
-        psum = ctx.enter_context(tc.psum_pool(name="psum", bufs=8))
+        out_pool = ctx.enter_context(tc.tile_pool(name="out_pool", bufs=4))
+        psum_t = ctx.enter_context(tc.psum_pool(name="psum_t", bufs=2))
+        psum_1 = ctx.enter_context(tc.psum_pool(name="psum_1", bufs=4))
+        psum_2 = ctx.enter_context(tc.psum_pool(name="psum_2", bufs=2))
 
         def load_x(u):
             b, s = divmod(u, 2)
@@ -62,13 +59,13 @@ def tile_rvnn_pa_t_kernel(
         x_tiles.append(load_x(1))
         wp_raw = load_first_weight(Wp2, "wp_raw")
         x_tiles.append(load_x(2))
-        x_tiles.append(load_x(3))
         wl_raw = const.tile([P, 2, PACK, WIDTH], BF16, name="wl_raw")
         nc.sync.dma_start(out=wl_raw[:], in_=Wl1.rearrange("(g p j) c -> p g j c", g=2, j=PACK))
-        for u in range(4, N_UNITS):
+        for u in range(3, N_UNITS):
             x_tiles.append(load_x(u))
 
         slopes = []
+        signs = []
         biases = []
         with nc.allow_non_contiguous_dma(reason="a few small vectors, once"):
             for s, (a_in, b_in) in enumerate(((ac, bc2), (ap, bp2))):
@@ -78,9 +75,18 @@ def tile_rvnn_pa_t_kernel(
                 nc.scalar.dma_start(out=b_bf[:], in_=b_in.rearrange("(p t) -> p t", t=PACK))
                 a_f = const.tile([P, 1], F32, name="a_f%d" % s)
                 nc.vector.tensor_copy(out=a_f[:], in_=a_bf[:])
+                above = const.tile([P, 1], F32, name="above%d" % s)
+                nc.vector.tensor_scalar(
+                    out=above[:], in0=a_f[:], scalar1=1.0, scalar2=-2.0, op0=ALU.is_gt, op1=ALU.mult
+                )
+                sign = const.tile([P, 1], F32, name="sign%d" % s)
+                nc.vector.tensor_scalar(
+                    out=sign[:], in0=above[:], scalar1=1.0, scalar2=None, op0=ALU.add
+                )
                 b_f = const.tile([P, PACK], F32, name="b_f%d" % s)
                 nc.vector.tensor_copy(out=b_f[:], in_=b_bf[:])
                 slopes.append(a_f)
+                signs.append(sign)
                 biases.append(b_f)
             bl_all = const.tile([P, WIDTH], BF16, name="bl_all")
             nc.scalar.dma_start(out=bl_all[:], in_=bl1.partition_broadcast(P))
@@ -91,6 +97,11 @@ def tile_rvnn_pa_t_kernel(
         warm = const.tile([P, 1], F32, name="warm")
         nc.vector.memset(warm[:], 0.0)
         nc.scalar.activation(out=warm[:], in_=warm[:], func=ACT.Tanh)
+
+        def gpsimd_copy(out, in_):
+            nc.gpsimd.tensor_scalar(
+                out=out, in0=in_, scalar1=1.0, scalar2=0.0, op0=ALU.mult, op1=ALU.add
+            )
 
         def regroup_weight(n, copy):
             grouped = const.tile([P, WIDTH, PACK], BF16, name="w_grouped%d" % n, align_bytes=64)
@@ -109,53 +120,62 @@ def tile_rvnn_pa_t_kernel(
             nc.vector.quantize_mx(out=codes[:].bitcast(FP8X4), scales=scales[:], in_=values)
             return codes, scales
 
-        def transpose_unit(h):
-            words = h[:].bitcast(F32).rearrange("p (a w) -> p a w", a=ROW_TILES)
+        def orient(u):
+            x = x_tiles[u]
+            nc.vector.tensor_scalar(
+                out=x[:], in0=x[:], scalar1=signs[u % 2][:, 0:1], scalar2=None, op0=ALU.mult
+            )
+
+        def transpose_unit(u):
+            words = x_tiles[u][:].rearrange("p a k -> p (a k)").bitcast(F32)
+            words = words.rearrange("p (a w) -> p a w", a=ROW_TILES)
             banks = []
             for half in range(2):
-                bank = psum.tile([P, 4, P], F32, tag="bank")
+                bank = psum_t.tile([P, 2, 2 * P], F32, tag="xt")
                 for a in range(2):
                     for h in range(2):
                         nc.tensor.transpose(
-                            bank[:, 2 * a + h, :],
+                            bank[:, h, a * P : (a + 1) * P],
                             words[:, 2 * half + a, h * P : (h + 1) * P],
                             ident[:],
                         )
                 banks.append(bank)
             return banks
 
-        def copy_out(banks):
-            ht = work.tile([P, BLOCK * PACK], BF16, tag="ht", align_bytes=64)
-            ht_words = ht[:].bitcast(F32).rearrange("p (a r h) -> p a r h", a=ROW_TILES, h=2)
-            for half in range(2):
-                nc.scalar.copy(
-                    out=ht_words[:, 2 * half : 2 * half + 2, :, :],
-                    in_=banks[half][:].rearrange("p (a h) r -> p a r h", h=2),
-                )
-            return ht
+        def bank_values(bank):
+            flat = bank[:].rearrange("p h q -> p (h q)").bitcast(BF16)
+            return flat.rearrange("p (h q e) -> p q h e", h=2, e=2)
 
-        def prelu_parts(u):
-            xt = x_tiles[u][:].rearrange("p a k -> p (a k)")
-            pos = work.tile([P, BLOCK * PACK], BF16, tag="pos", align_bytes=64)
-            neg = work.tile([P, BLOCK * PACK], BF16, tag="neg", align_bytes=64)
-            nc.vector.tensor_scalar(
-                out=pos[:], in0=xt, scalar1=0.0, scalar2=None, op0=ALU.max
-            )
-            nc.vector.tensor_scalar(
-                out=neg[:], in0=xt, scalar1=0.0, scalar2=slopes[u % 2][:, 0:1],
-                op0=ALU.min, op1=ALU.mult,
-            )
-            return pos, neg
+        def as_rows(flat):
+            return flat.rearrange("p (q h e) -> p q h e", h=2, e=2)
 
-        def prelu_join(pos, neg):
-            nc.vector.tensor_tensor(out=pos[:], in0=pos[:], in1=neg[:], op=ALU.add)
-            return pos
+        def scaled_on_vector(u, bank):
+            y = work.tile([P, 2 * WIDTH], BF16, tag="yv")
+            nc.vector.tensor_scalar(
+                out=as_rows(y[:]), in0=bank_values(bank), scalar1=slopes[u % 2][:, 0:1],
+                scalar2=None, op0=ALU.mult,
+            )
+            return y
+
+        def scaled_on_scalar(u, bank):
+            y = work.tile([P, 2 * WIDTH], BF16, tag="ys")
+            nc.scalar.activation(
+                out=as_rows(y[:]), in_=bank_values(bank), func=ACT.Copy,
+                scale=slopes[u % 2][:, 0:1],
+            )
+            return y
+
+        def larger(ht, half, bank, y):
+            nc.vector.tensor_tensor(
+                out=as_rows(ht[:, half * 1024 : (half + 1) * 1024]),
+                in0=bank_values(bank), in1=as_rows(y[:]), op=ALU.max,
+            )
 
         def first_layer_matmuls(u, h):
             s = u % 2
             accs = []
             for t in range(PACK):
-                acc = psum.tile([P, BLOCK], F32, tag="bank")
+                acc = psum_1.tile([P, BLOCK], F32, tag="acc1")
                 cols = slice(t * P, (t + 1) * P)
                 nc.tensor.matmul_mx(
                     out=acc[:],
@@ -174,21 +194,15 @@ def tile_rvnn_pa_t_kernel(
             for t in range(PACK):
                 nc.scalar.activation(
                     out=planes[:, t, :], in_=accs[t][:], func=ACT.Tanh,
-                    bias=biases[u % 2][:, t : t + 1], scale=1.0,
+                    bias=biases[u % 2][:, t : t + 1], scale=signs[u % 2][:, 0:1],
                 )
             return planes
-
-        def regroup(copy, grouped, planes, cols):
-            copy(
-                out=grouped[:, cols, :].rearrange("p (c i) t -> p c t i", i=4),
-                in_=planes[:, :, cols].rearrange("p t (c i) -> p c t i", i=4),
-            )
 
         def second_layer_matmuls(n):
             b, half = divmod(n, 2)
             accs = []
             for a in (2 * half, 2 * half + 1):
-                acc = psum.tile([P, WIDTH], F32, tag="bank")
+                acc = psum_2.tile([P, WIDTH], F32, tag="acc2")
                 cols = slice(a * P, (a + 1) * P)
                 for g in range(2):
                     nc.tensor.matmul_mx(
@@ -204,27 +218,21 @@ def tile_rvnn_pa_t_kernel(
             return accs
 
         def add_bias(accs):
-            sums = []
-            for acc in accs:
-                total = out_pool.tile([P, WIDTH], F32, tag="total")
-                nc.vector.tensor_tensor(out=total[:], in0=acc[:], in1=bl_all[:], op=ALU.add)
-                sums.append(total)
-            return sums
+            total = out_pool.tile([P, 2, WIDTH], F32, tag="total")
+            for k in range(2):
+                nc.vector.tensor_tensor(out=total[:, k, :], in0=accs[k][:], in1=bl_all[:], op=ALU.add)
+            return total
 
-        def finish(n, sums):
+        def finish(n, total):
             b, half = divmod(n, 2)
             rows = out[b * BLOCK : (b + 1) * BLOCK, :].rearrange("(p a) c -> p a c", a=ROW_TILES)
-            for k in range(2):
-                nc.scalar.activation(out=sums[k][:], in_=sums[k][:], func=ACT.Tanh)
-                nc.sync.dma_start(out=rows[:, 2 * half + k, :], in_=sums[k][:])
+            nc.scalar.activation(out=total[:], in_=total[:], func=ACT.Tanh)
+            nc.sync.dma_start(out=rows[:, 2 * half : 2 * half + 2, :], in_=total[:])
 
         def is_unit(u):
             return 0 <= u < N_UNITS
 
-        h_of = {}
         banks_of = {}
-        ht_of = {}
-        parts_of = {}
         h_q = {}
         accs1_of = {}
         planes_of = {}
@@ -235,53 +243,53 @@ def tile_rvnn_pa_t_kernel(
         w_grouped = {}
         w_q = {}
         with tc.manual_schedule():
-            for i in range(N_UNITS + 11):
-                if is_unit(i - 9):
-                    sums_of[i - 9] = add_bias(accs2_of[i - 9])
-                if is_unit(i - 3):
-                    accs1_of[i - 3] = first_layer_matmuls(i - 3, h_q[i - 3])
-                if is_unit(i - 5):
-                    regroup(
-                        nc.scalar.copy, grouped_of[i - 5], planes_of[i - 5],
-                        slice(VECTOR_COLS, VECTOR_COLS + SCALAR_COLS),
-                    )
-                if is_unit(i - 10):
-                    finish(i - 10, sums_of[i - 10])
-                if is_unit(i - 5):
-                    nc.gpsimd.tensor_scalar(
-                        out=grouped_of[i - 5][:, VECTOR_COLS + SCALAR_COLS :, :],
-                        in0=planes_of[i - 5][:, :, VECTOR_COLS + SCALAR_COLS :].rearrange(
-                            "p t c -> p c t"
-                        ),
-                        scalar1=1.0, scalar2=0.0, op0=ALU.mult, op1=ALU.add,
-                    )
-                if is_unit(i - 3):
-                    planes_of[i - 3] = first_layer_tanh(i - 3, accs1_of[i - 3])
-                if is_unit(i):
-                    parts_of[i] = prelu_parts(i)
-                if is_unit(i - 1):
-                    banks_of[i - 1] = transpose_unit(h_of[i - 1])
-                if is_unit(i - 8):
-                    accs2_of[i - 8] = second_layer_matmuls(i - 8)
+            for i in range(N_UNITS + 8):
                 if is_unit(i - 2):
-                    h_q[i - 2] = quantise(ht_of[i - 2][:], "h")
-                if is_unit(i - 1):
-                    ht_of[i - 1] = copy_out(banks_of[i - 1])
-                if is_unit(i):
-                    h_of[i] = prelu_join(parts_of[i][0], parts_of[i][1])
-                if is_unit(i - 4):
-                    grouped_of[i - 4] = work.tile(
+                    accs1_of[i - 2] = first_layer_matmuls(i - 2, h_q[i - 2])
+                if i == 1:
+                    w_grouped[2] = regroup_weight(2, gpsimd_copy)
+                if is_unit(i - 3):
+                    grouped_of[i - 3] = work.tile(
                         [P, BLOCK, PACK], BF16, tag="z_grouped", name="z_grouped", align_bytes=64
                     )
-                    regroup(
-                        nc.vector.tensor_copy, grouped_of[i - 4], planes_of[i - 4],
-                        slice(0, VECTOR_COLS),
+                    gpsimd_copy(
+                        out=grouped_of[i - 3][:], in_=planes_of[i - 3][:].rearrange("p t c -> p c t")
                     )
+                if is_unit(i - 7):
+                    finish(i - 7, sums_of[i - 7])
+                if is_unit(i - 1):
+                    y_s = scaled_on_scalar(i - 1, banks_of[i - 1][1])
+                if i == 1:
+                    w_grouped[1] = regroup_weight(1, nc.scalar.copy)
+                if is_unit(i):
+                    orient(i)
+                if i == 0:
+                    w_grouped[0] = regroup_weight(0, nc.vector.tensor_copy)
+                if i == 2:
+                    w_q[1] = quantise(w_grouped[1][:].rearrange("p c j -> p (c j)"), "w")
+                    w_grouped[3] = regroup_weight(3, nc.vector.tensor_copy)
+                if is_unit(i - 1):
+                    y_v = scaled_on_vector(i - 1, banks_of[i - 1][0])
+                if i == 1:
+                    w_q[0] = quantise(w_grouped[0][:].rearrange("p c j -> p (c j)"), "w")
+                if i == 3:
+                    w_q[2] = quantise(w_grouped[2][:].rearrange("p c j -> p (c j)"), "w")
+                    w_q[3] = quantise(w_grouped[3][:].rearrange("p c j -> p (c j)"), "w")
+                if is_unit(i - 6):
+                    sums_of[i - 6] = add_bias(accs2_of[i - 6])
+                if is_unit(i - 1):
+                    ht = work.tile([P, BLOCK * PACK], BF16, tag="ht", align_bytes=64)
+                    larger(ht, 0, banks_of[i - 1][0], y_v)
+                    larger(ht, 1, banks_of[i - 1][1], y_s)
+                if is_unit(i - 3):
+                    z_q[i - 3] = quantise(
+                        grouped_of[i - 3][:].rearrange("p c t -> p (c t)"), "z", bufs=8
+                    )
+                if is_unit(i - 1):
+                    h_q[i - 1] = quantise(ht[:], "h")
+                if is_unit(i - 2):
+                    planes_of[i - 2] = first_layer_tanh(i - 2, accs1_of[i - 2])
                 if is_unit(i - 5):
-                    z_q[i - 5] = quantise(
-                        grouped_of[i - 5][:].rearrange("p c t -> p (c t)"), "z", bufs=8
-                    )
-                if i < 4:
-                    w_grouped[i] = regroup_weight(i, nc.scalar.copy)
-                if 1 <= i <= 4:
-                    w_q[i - 1] = quantise(w_grouped[i - 1][:].rearrange("p c j -> p (c j)"), "w")
+                    accs2_of[i - 5] = second_layer_matmuls(i - 5)
+                if is_unit(i):
+                    banks_of[i] = transpose_unit(i)

@@ -35,9 +35,8 @@ def tile_rvnn_pa_t_kernel(
         work = ctx.enter_context(tc.tile_pool(name="work", bufs=3))
         codes_pool = ctx.enter_context(tc.tile_pool(name="codes_pool", bufs=4))
         out_pool = ctx.enter_context(tc.tile_pool(name="out_pool", bufs=4))
-        psum_t = ctx.enter_context(tc.psum_pool(name="psum_t", bufs=2))
         psum_1 = ctx.enter_context(tc.psum_pool(name="psum_1", bufs=4))
-        psum_2 = ctx.enter_context(tc.psum_pool(name="psum_2", bufs=2))
+        psum_2 = ctx.enter_context(tc.psum_pool(name="psum_2", bufs=4))
 
         def load_x(u):
             b, s = divmod(u, 2)
@@ -54,6 +53,12 @@ def tile_rvnn_pa_t_kernel(
             )
             return raw
 
+        slopes_bf = []
+        with nc.allow_non_contiguous_dma(reason="a few small vectors, once"):
+            for s, a_in in enumerate((ac, ap)):
+                a_bf = const.tile([P, 1], BF16, name="a_bf%d" % s)
+                nc.sync.dma_start(out=a_bf[:], in_=a_in.partition_broadcast(P))
+                slopes_bf.append(a_bf)
         x_tiles = [load_x(0)]
         wc_raw = load_first_weight(Wc2, "wc_raw")
         x_tiles.append(load_x(1))
@@ -61,42 +66,43 @@ def tile_rvnn_pa_t_kernel(
         x_tiles.append(load_x(2))
         wl_raw = const.tile([P, 2, PACK, WIDTH], BF16, name="wl_raw")
         nc.sync.dma_start(out=wl_raw[:], in_=Wl1.rearrange("(g p j) c -> p g j c", g=2, j=PACK))
-        for u in range(3, N_UNITS):
+        for u in range(3, 8):
+            x_tiles.append(load_x(u))
+        bl_all = const.tile([P, WIDTH], BF16, name="bl_all")
+        with nc.allow_non_contiguous_dma(reason="one small vector, once"):
+            nc.sync.dma_start(out=bl_all[:], in_=bl1.partition_broadcast(P))
+        for u in range(8, N_UNITS):
             x_tiles.append(load_x(u))
 
-        slopes = []
-        signs = []
-        biases = []
+        biases_bf = []
         with nc.allow_non_contiguous_dma(reason="a few small vectors, once"):
-            for s, (a_in, b_in) in enumerate(((ac, bc2), (ap, bp2))):
-                a_bf = const.tile([P, 1], BF16, name="a_bf%d" % s)
-                nc.scalar.dma_start(out=a_bf[:], in_=a_in.partition_broadcast(P))
+            for s, b_in in enumerate((bc2, bp2)):
                 b_bf = const.tile([P, PACK], BF16, name="b_bf%d" % s)
                 nc.scalar.dma_start(out=b_bf[:], in_=b_in.rearrange("(p t) -> p t", t=PACK))
-                a_f = const.tile([P, 1], F32, name="a_f%d" % s)
-                nc.vector.tensor_copy(out=a_f[:], in_=a_bf[:])
-                above = const.tile([P, 1], F32, name="above%d" % s)
-                nc.vector.tensor_scalar(
-                    out=above[:], in0=a_f[:], scalar1=1.0, scalar2=-2.0, op0=ALU.is_gt, op1=ALU.mult
-                )
-                sign = const.tile([P, 1], F32, name="sign%d" % s)
-                nc.vector.tensor_scalar(
-                    out=sign[:], in0=above[:], scalar1=1.0, scalar2=None, op0=ALU.add
-                )
-                b_f = const.tile([P, PACK], F32, name="b_f%d" % s)
-                nc.vector.tensor_copy(out=b_f[:], in_=b_bf[:])
-                slopes.append(a_f)
-                signs.append(sign)
-                biases.append(b_f)
-            bl_all = const.tile([P, WIDTH], BF16, name="bl_all")
-            nc.scalar.dma_start(out=bl_all[:], in_=bl1.partition_broadcast(P))
-
-        ident = const.tile([P, P], F32, name="ident")
-        make_identity(nc, ident[:])
+                biases_bf.append(b_bf)
 
         warm = const.tile([P, 1], F32, name="warm")
         nc.vector.memset(warm[:], 0.0)
         nc.scalar.activation(out=warm[:], in_=warm[:], func=ACT.Tanh)
+
+        above = [const.tile([P, 1], F32, name="above%d" % s) for s in range(2)]
+        signs = [const.tile([P, 1], F32, name="sign%d" % s) for s in range(2)]
+        slopes = [const.tile([P, 1], F32, name="a_f%d" % s) for s in range(2)]
+        biases = [const.tile([P, PACK], F32, name="b_f%d" % s) for s in range(2)]
+        for s in range(2):
+            nc.vector.tensor_scalar(
+                out=above[s][:], in0=slopes_bf[s][:], scalar1=1.0, scalar2=-2.0,
+                op0=ALU.is_gt, op1=ALU.mult,
+            )
+        for s in range(2):
+            nc.vector.tensor_scalar(
+                out=signs[s][:], in0=above[s][:], scalar1=1.0, scalar2=None, op0=ALU.add
+            )
+        for s in range(2):
+            nc.vector.tensor_copy(out=slopes[s][:], in_=slopes_bf[s][:])
+
+        ident = const.tile([P, P], F32, name="ident")
+        make_identity(nc, ident[:])
 
         def gpsimd_copy(out, in_):
             nc.gpsimd.tensor_scalar(
@@ -131,7 +137,7 @@ def tile_rvnn_pa_t_kernel(
             words = words.rearrange("p (a w) -> p a w", a=ROW_TILES)
             banks = []
             for half in range(2):
-                bank = psum_t.tile([P, 2, 2 * P], F32, tag="xt")
+                bank = psum_2.tile([P, 2, 2 * P], F32, tag="bank")
                 for a in range(2):
                     for h in range(2):
                         nc.tensor.transpose(
@@ -202,7 +208,7 @@ def tile_rvnn_pa_t_kernel(
             b, half = divmod(n, 2)
             accs = []
             for a in (2 * half, 2 * half + 1):
-                acc = psum_2.tile([P, WIDTH], F32, tag="acc2")
+                acc = psum_2.tile([P, WIDTH], F32, tag="bank")
                 cols = slice(a * P, (a + 1) * P)
                 for g in range(2):
                     nc.tensor.matmul_mx(
@@ -226,11 +232,30 @@ def tile_rvnn_pa_t_kernel(
         def finish(n, total):
             b, half = divmod(n, 2)
             rows = out[b * BLOCK : (b + 1) * BLOCK, :].rearrange("(p a) c -> p a c", a=ROW_TILES)
-            nc.scalar.activation(out=total[:], in_=total[:], func=ACT.Tanh)
-            nc.sync.dma_start(out=rows[:, 2 * half : 2 * half + 2, :], in_=total[:])
+            pieces = (slice(0, 1), slice(1, 2)) if n == N_UNITS - 1 else (slice(0, 2),)
+            for part in pieces:
+                nc.scalar.activation(out=total[:, part, :], in_=total[:, part, :], func=ACT.Tanh)
+                nc.sync.dma_start(
+                    out=rows[:, 2 * half + part.start : 2 * half + part.stop, :],
+                    in_=total[:, part, :],
+                )
 
         def is_unit(u):
             return 0 <= u < N_UNITS
+
+        def regroup(copy, grouped, planes, cols):
+            copy(
+                out=grouped[:, cols, :].rearrange("p (c i) t -> p c t i", i=4),
+                in_=planes[:, :, cols].rearrange("p t (c i) -> p c t i", i=4),
+            )
+
+        def new_grouped():
+            return work.tile(
+                [P, BLOCK, PACK], BF16, tag="z_grouped", name="z_grouped", align_bytes=64
+            )
+
+        def flat(grouped):
+            return grouped[:].rearrange("p c t -> p (c t)")
 
         banks_of = {}
         h_q = {}
@@ -242,16 +267,15 @@ def tile_rvnn_pa_t_kernel(
         sums_of = {}
         w_grouped = {}
         w_q = {}
+        last = N_UNITS - 1
         with tc.manual_schedule():
-            for i in range(N_UNITS + 8):
+            for i in range(N_UNITS + 2):
                 if is_unit(i - 2):
                     accs1_of[i - 2] = first_layer_matmuls(i - 2, h_q[i - 2])
                 if i == 1:
                     w_grouped[2] = regroup_weight(2, gpsimd_copy)
                 if is_unit(i - 3):
-                    grouped_of[i - 3] = work.tile(
-                        [P, BLOCK, PACK], BF16, tag="z_grouped", name="z_grouped", align_bytes=64
-                    )
+                    grouped_of[i - 3] = new_grouped()
                     gpsimd_copy(
                         out=grouped_of[i - 3][:], in_=planes_of[i - 3][:].rearrange("p t c -> p c t")
                     )
@@ -266,15 +290,17 @@ def tile_rvnn_pa_t_kernel(
                 if i == 0:
                     w_grouped[0] = regroup_weight(0, nc.vector.tensor_copy)
                 if i == 2:
-                    w_q[1] = quantise(w_grouped[1][:].rearrange("p c j -> p (c j)"), "w")
+                    w_q[1] = quantise(flat(w_grouped[1]), "w")
                     w_grouped[3] = regroup_weight(3, nc.vector.tensor_copy)
                 if is_unit(i - 1):
                     y_v = scaled_on_vector(i - 1, banks_of[i - 1][0])
                 if i == 1:
-                    w_q[0] = quantise(w_grouped[0][:].rearrange("p c j -> p (c j)"), "w")
+                    w_q[0] = quantise(flat(w_grouped[0]), "w")
+                    for s in range(2):
+                        nc.vector.tensor_copy(out=biases[s][:], in_=biases_bf[s][:])
                 if i == 3:
-                    w_q[2] = quantise(w_grouped[2][:].rearrange("p c j -> p (c j)"), "w")
-                    w_q[3] = quantise(w_grouped[3][:].rearrange("p c j -> p (c j)"), "w")
+                    w_q[2] = quantise(flat(w_grouped[2]), "w")
+                    w_q[3] = quantise(flat(w_grouped[3]), "w")
                 if is_unit(i - 6):
                     sums_of[i - 6] = add_bias(accs2_of[i - 6])
                 if is_unit(i - 1):
@@ -282,9 +308,7 @@ def tile_rvnn_pa_t_kernel(
                     larger(ht, 0, banks_of[i - 1][0], y_v)
                     larger(ht, 1, banks_of[i - 1][1], y_s)
                 if is_unit(i - 3):
-                    z_q[i - 3] = quantise(
-                        grouped_of[i - 3][:].rearrange("p c t -> p (c t)"), "z", bufs=8
-                    )
+                    z_q[i - 3] = quantise(flat(grouped_of[i - 3]), "z", bufs=8)
                 if is_unit(i - 1):
                     h_q[i - 1] = quantise(ht[:], "h")
                 if is_unit(i - 2):
@@ -293,3 +317,33 @@ def tile_rvnn_pa_t_kernel(
                     accs2_of[i - 5] = second_layer_matmuls(i - 5)
                 if is_unit(i):
                     banks_of[i] = transpose_unit(i)
+
+            accs2_of[last - 2] = second_layer_matmuls(last - 2)
+            for n in (last - 3, last - 2):
+                sums_of[n] = add_bias(accs2_of[n])
+            grouped_of[last] = new_grouped()
+            regroup(gpsimd_copy, grouped_of[last], planes_of[last], slice(384, 512))
+            codes = codes_pool.tile(
+                [P, BLOCK], U32, tag="z_codes", name="last_codes", bufs=8, align_bytes=64
+            )
+            scales = codes_pool.tile(
+                [P, BLOCK], U8, tag="z_scales", name="last_scales", bufs=8, align_bytes=64
+            )
+            z_q[last] = (codes, scales)
+
+            def quantise_last(cols):
+                nc.vector.quantize_mx(
+                    out=codes[:, cols].bitcast(FP8X4), scales=scales[:, cols],
+                    in_=grouped_of[last][:, cols, :].rearrange("p c t -> p (c t)"),
+                )
+
+            regroup(nc.vector.tensor_copy, grouped_of[last], planes_of[last], slice(0, 256))
+            regroup(nc.vector.tensor_copy, grouped_of[last], planes_of[last], slice(256, 384))
+            quantise_last(slice(0, 256))
+            quantise_last(slice(256, 512))
+            for n in range(last - 4, last - 1):
+                finish(n, sums_of[n])
+            for n in (last - 1, last):
+                accs2_of[n] = second_layer_matmuls(n)
+                sums_of[n] = add_bias(accs2_of[n])
+                finish(n, sums_of[n])

@@ -38,11 +38,15 @@ def tile_rvnn_pa_t_kernel(
         psum_1 = ctx.enter_context(tc.psum_pool(name="psum_1", bufs=4))
         psum_2 = ctx.enter_context(tc.psum_pool(name="psum_2", bufs=4))
 
+        first_halves = (slice(0, 2), slice(2, 4))
+
         def load_x(u):
             b, s = divmod(u, 2)
             x = x_pool.tile([P, ROW_TILES, WIDTH], BF16, tag="x", name="x%d" % u)
             rows = streams[s][b * BLOCK : (b + 1) * BLOCK, :]
-            nc.sync.dma_start(out=x[:], in_=rows.rearrange("(p a) k -> p a k", a=ROW_TILES))
+            rows = rows.rearrange("(p a) k -> p a k", a=ROW_TILES)
+            for part in first_halves if u == 0 else (slice(0, ROW_TILES),):
+                nc.sync.dma_start(out=x[:, part, :], in_=rows[:, part, :])
             return x
 
         def load_first_weight(w, name):
@@ -109,16 +113,23 @@ def tile_rvnn_pa_t_kernel(
                 out=out, in0=in_, scalar1=1.0, scalar2=0.0, op0=ALU.mult, op1=ALU.add
             )
 
-        def regroup_weight(n, copy):
-            grouped = const.tile([P, WIDTH, PACK], BF16, name="w_grouped%d" % n, align_bytes=64)
-            if n < 2:
+        w_grouped = [
+            const.tile([P, WIDTH, PACK], BF16, name="w_grouped%d" % n, align_bytes=64)
+            for n in range(4)
+        ]
+
+        def regroup_first_weight(n, copy, t0, t1):
+            for t in range(t0, t1):
                 copy(
-                    out=grouped[:].rearrange("p (t q) j -> p t q j", t=PACK),
-                    in_=(wc_raw, wp_raw)[n][:].rearrange("p j (q t) -> p t q j", t=PACK),
+                    out=w_grouped[n][:, t * P : (t + 1) * P, :],
+                    in_=(wc_raw, wp_raw)[n][:].rearrange("p j (q t) -> p t q j", t=PACK)[:, t, :, :],
                 )
-            else:
-                copy(out=grouped[:], in_=wl_raw[:, n - 2, :, :].rearrange("p j c -> p c j"))
-            return grouped
+
+        def regroup_second_weight(n, copy, cols):
+            copy(
+                out=w_grouped[n][:, cols, :].rearrange("p (c i) j -> p c j i", i=4),
+                in_=wl_raw[:, n - 2, :, cols].rearrange("p j (c i) -> p c j i", i=4),
+            )
 
         def quantise(values, tag, bufs=4):
             codes = codes_pool.tile([P, BLOCK], U32, tag=tag + "_codes", bufs=bufs, align_bytes=64)
@@ -127,10 +138,11 @@ def tile_rvnn_pa_t_kernel(
             return codes, scales
 
         def orient(u):
-            x = x_tiles[u]
-            nc.vector.tensor_scalar(
-                out=x[:], in0=x[:], scalar1=signs[u % 2][:, 0:1], scalar2=None, op0=ALU.mult
-            )
+            for part in first_halves if u == 0 else (slice(0, ROW_TILES),):
+                x = x_tiles[u][:, part, :]
+                nc.vector.tensor_scalar(
+                    out=x, in0=x, scalar1=signs[u % 2][:, 0:1], scalar2=None, op0=ALU.mult
+                )
 
         def transpose_unit(u):
             words = x_tiles[u][:].rearrange("p a k -> p (a k)").bitcast(F32)
@@ -243,10 +255,15 @@ def tile_rvnn_pa_t_kernel(
         def is_unit(u):
             return 0 <= u < N_UNITS
 
-        def regroup(copy, grouped, planes, cols):
+        def regroup(copy, u, cols):
             copy(
-                out=grouped[:, cols, :].rearrange("p (c i) t -> p c t i", i=4),
-                in_=planes[:, :, cols].rearrange("p t (c i) -> p c t i", i=4),
+                out=grouped_of[u][:, cols, :].rearrange("p (c i) t -> p c t i", i=4),
+                in_=planes_of[u][:, :, cols].rearrange("p t (c i) -> p c t i", i=4),
+            )
+
+        def gpsimd_regroup(u, cols):
+            gpsimd_copy(
+                out=grouped_of[u][:, cols, :], in_=planes_of[u][:, :, cols].rearrange("p t c -> p c t")
             )
 
         def new_grouped():
@@ -257,6 +274,9 @@ def tile_rvnn_pa_t_kernel(
         def flat(grouped):
             return grouped[:].rearrange("p c t -> p (c t)")
 
+        def new_ht():
+            return work.tile([P, BLOCK * PACK], BF16, tag="ht", name="ht", align_bytes=64)
+
         banks_of = {}
         h_q = {}
         accs1_of = {}
@@ -265,49 +285,65 @@ def tile_rvnn_pa_t_kernel(
         z_q = {}
         accs2_of = {}
         sums_of = {}
-        w_grouped = {}
         w_q = {}
         last = N_UNITS - 1
         with tc.manual_schedule():
-            for i in range(N_UNITS + 2):
+            orient(0)
+            banks_of[0] = transpose_unit(0)
+            regroup_first_weight(0, nc.scalar.copy, 0, 3)
+            regroup_first_weight(0, gpsimd_copy, 3, 4)
+            y_v = scaled_on_vector(0, banks_of[0][0])
+            orient(1)
+            banks_of[1] = transpose_unit(1)
+            y_s = scaled_on_vector(0, banks_of[0][1])
+            ht = new_ht()
+            larger(ht, 0, banks_of[0][0], y_v)
+            larger(ht, 1, banks_of[0][1], y_s)
+            w_q[0] = quantise(flat(w_grouped[0]), "w")
+            h_q[0] = quantise(ht[:], "h")
+            for s in range(2):
+                nc.vector.tensor_copy(out=biases[s][:], in_=biases_bf[s][:])
+            for i in range(2, N_UNITS + 2):
                 if is_unit(i - 2):
                     accs1_of[i - 2] = first_layer_matmuls(i - 2, h_q[i - 2])
-                if i == 1:
-                    w_grouped[2] = regroup_weight(2, gpsimd_copy)
+                if i == 2:
+                    regroup_first_weight(1, gpsimd_copy, 2, 4)
                 if is_unit(i - 3):
                     grouped_of[i - 3] = new_grouped()
+                    if i - 3 < 14:
+                        gpsimd_regroup(i - 3, slice(0, BLOCK))
+                    else:
+                        gpsimd_regroup(i - 3, slice(0, 256))
+                if i in (2, 4):
                     gpsimd_copy(
-                        out=grouped_of[i - 3][:], in_=planes_of[i - 3][:].rearrange("p t c -> p c t")
+                        out=w_grouped[2 if i == 2 else 3][:],
+                        in_=wl_raw[:, 0 if i == 2 else 1, :, :].rearrange("p j c -> p c j"),
                     )
                 if is_unit(i - 7):
                     finish(i - 7, sums_of[i - 7])
                 if is_unit(i - 1):
                     y_s = scaled_on_scalar(i - 1, banks_of[i - 1][1])
-                if i == 1:
-                    w_grouped[1] = regroup_weight(1, nc.scalar.copy)
                 if is_unit(i):
                     orient(i)
-                if i == 0:
-                    w_grouped[0] = regroup_weight(0, nc.vector.tensor_copy)
-                if i == 2:
-                    w_q[1] = quantise(flat(w_grouped[1]), "w")
-                    w_grouped[3] = regroup_weight(3, nc.vector.tensor_copy)
                 if is_unit(i - 1):
                     y_v = scaled_on_vector(i - 1, banks_of[i - 1][0])
-                if i == 1:
-                    w_q[0] = quantise(flat(w_grouped[0]), "w")
-                    for s in range(2):
-                        nc.vector.tensor_copy(out=biases[s][:], in_=biases_bf[s][:])
-                if i == 3:
-                    w_q[2] = quantise(flat(w_grouped[2]), "w")
-                    w_q[3] = quantise(flat(w_grouped[3]), "w")
+                if i == 2:
+                    regroup_first_weight(1, nc.vector.tensor_copy, 0, 2)
                 if is_unit(i - 6):
                     sums_of[i - 6] = add_bias(accs2_of[i - 6])
                 if is_unit(i - 1):
-                    ht = work.tile([P, BLOCK * PACK], BF16, tag="ht", align_bytes=64)
+                    ht = new_ht()
                     larger(ht, 0, banks_of[i - 1][0], y_v)
                     larger(ht, 1, banks_of[i - 1][1], y_s)
+                if i == 2:
+                    w_q[1] = quantise(flat(w_grouped[1]), "w")
+                if i - 1 in (2, 4):
+                    w_q[2 if i - 1 == 2 else 3] = quantise(
+                        flat(w_grouped[2 if i - 1 == 2 else 3]), "w"
+                    )
                 if is_unit(i - 3):
+                    if i - 3 >= 14:
+                        regroup(nc.vector.tensor_copy, i - 3, slice(256, BLOCK))
                     z_q[i - 3] = quantise(flat(grouped_of[i - 3]), "z", bufs=8)
                 if is_unit(i - 1):
                     h_q[i - 1] = quantise(ht[:], "h")
@@ -315,14 +351,13 @@ def tile_rvnn_pa_t_kernel(
                     planes_of[i - 2] = first_layer_tanh(i - 2, accs1_of[i - 2])
                 if is_unit(i - 5):
                     accs2_of[i - 5] = second_layer_matmuls(i - 5)
-                if is_unit(i):
+                if 2 <= i < N_UNITS:
                     banks_of[i] = transpose_unit(i)
 
             accs2_of[last - 2] = second_layer_matmuls(last - 2)
-            for n in (last - 3, last - 2):
-                sums_of[n] = add_bias(accs2_of[n])
+            sums_of[last - 3] = add_bias(accs2_of[last - 3])
             grouped_of[last] = new_grouped()
-            regroup(gpsimd_copy, grouped_of[last], planes_of[last], slice(384, 512))
+            gpsimd_regroup(last, slice(384, 512))
             codes = codes_pool.tile(
                 [P, BLOCK], U32, tag="z_codes", name="last_codes", bufs=8, align_bytes=64
             )
@@ -337,10 +372,11 @@ def tile_rvnn_pa_t_kernel(
                     in_=grouped_of[last][:, cols, :].rearrange("p c t -> p (c t)"),
                 )
 
-            regroup(nc.vector.tensor_copy, grouped_of[last], planes_of[last], slice(0, 256))
-            regroup(nc.vector.tensor_copy, grouped_of[last], planes_of[last], slice(256, 384))
+            regroup(nc.vector.tensor_copy, last, slice(0, 256))
+            regroup(nc.vector.tensor_copy, last, slice(256, 384))
             quantise_last(slice(0, 256))
             quantise_last(slice(256, 512))
+            sums_of[last - 2] = add_bias(accs2_of[last - 2])
             for n in range(last - 4, last - 1):
                 finish(n, sums_of[n])
             for n in (last - 1, last):

@@ -268,7 +268,7 @@ def tile_rvnn_pa_t_kernel(
 
         def new_grouped():
             return work.tile(
-                [P, BLOCK, PACK], BF16, tag="z_grouped", name="z_grouped", align_bytes=64
+                [P, BLOCK, PACK], BF16, tag="z_grouped", name="z_grouped", bufs=1, align_bytes=64
             )
 
         def flat(grouped):
@@ -277,6 +277,12 @@ def tile_rvnn_pa_t_kernel(
         def new_ht():
             return work.tile([P, BLOCK * PACK], BF16, tag="ht", name="ht", align_bytes=64)
 
+        def gpsimd_cols(u):
+            if u < 3:
+                return 320
+            return 448 if u < 14 else 192
+
+        E1_ON_VECTOR = (0,)
         banks_of = {}
         h_q = {}
         accs1_of = {}
@@ -303,6 +309,7 @@ def tile_rvnn_pa_t_kernel(
             h_q[0] = quantise(ht[:], "h")
             for s in range(2):
                 nc.vector.tensor_copy(out=biases[s][:], in_=biases_bf[s][:])
+            orient(2)
             for i in range(2, N_UNITS + 2):
                 if is_unit(i - 2):
                     accs1_of[i - 2] = first_layer_matmuls(i - 2, h_q[i - 2])
@@ -310,25 +317,17 @@ def tile_rvnn_pa_t_kernel(
                     regroup_first_weight(1, gpsimd_copy, 2, 4)
                 if is_unit(i - 3):
                     grouped_of[i - 3] = new_grouped()
-                    if i - 3 < 14:
-                        gpsimd_regroup(i - 3, slice(0, BLOCK))
-                    else:
-                        gpsimd_regroup(i - 3, slice(0, 256))
-                if i in (2, 4):
-                    gpsimd_copy(
-                        out=w_grouped[2 if i == 2 else 3][:],
-                        in_=wl_raw[:, 0 if i == 2 else 1, :, :].rearrange("p j c -> p c j"),
-                    )
+                    g_cols = gpsimd_cols(i - 3)
+                    for c in range(0, g_cols, g_cols // 1):
+                        gpsimd_regroup(i - 3, slice(c, c + g_cols // 1))
                 if is_unit(i - 7):
                     finish(i - 7, sums_of[i - 7])
-                if is_unit(i - 1):
+                if is_unit(i - 1) and i - 1 not in E1_ON_VECTOR:
                     y_s = scaled_on_scalar(i - 1, banks_of[i - 1][1])
-                if is_unit(i):
-                    orient(i)
                 if is_unit(i - 1):
                     y_v = scaled_on_vector(i - 1, banks_of[i - 1][0])
-                if i == 2:
-                    regroup_first_weight(1, nc.vector.tensor_copy, 0, 2)
+                    if i - 1 in E1_ON_VECTOR:
+                        y_s = scaled_on_vector(i - 1, banks_of[i - 1][1])
                 if is_unit(i - 6):
                     sums_of[i - 6] = add_bias(accs2_of[i - 6])
                 if is_unit(i - 1):
@@ -336,19 +335,31 @@ def tile_rvnn_pa_t_kernel(
                     larger(ht, 0, banks_of[i - 1][0], y_v)
                     larger(ht, 1, banks_of[i - 1][1], y_s)
                 if i == 2:
+                    regroup_first_weight(1, nc.vector.tensor_copy, 0, 2)
+                if i == 4:
+                    regroup_second_weight(3, nc.vector.tensor_copy, slice(256, 512))
+                if i == 2:
                     w_q[1] = quantise(flat(w_grouped[1]), "w")
-                if i - 1 in (2, 4):
-                    w_q[2 if i - 1 == 2 else 3] = quantise(
-                        flat(w_grouped[2 if i - 1 == 2 else 3]), "w"
-                    )
-                if is_unit(i - 3):
-                    if i - 3 >= 14:
-                        regroup(nc.vector.tensor_copy, i - 3, slice(256, BLOCK))
-                    z_q[i - 3] = quantise(flat(grouped_of[i - 3]), "z", bufs=8)
+                if i == 4:
+                    w_q[2] = quantise(flat(w_grouped[2]), "w")
+                if i == 5:
+                    w_q[3] = quantise(flat(w_grouped[3]), "w")
+                if is_unit(i + 1):
+                    orient(i + 1)
+                if is_unit(i - 3) and g_cols < BLOCK:
+                    regroup(nc.vector.tensor_copy, i - 3, slice(g_cols, BLOCK))
                 if is_unit(i - 1):
                     h_q[i - 1] = quantise(ht[:], "h")
+                if is_unit(i - 3):
+                    z_q[i - 3] = quantise(flat(grouped_of[i - 3]), "z", bufs=8)
                 if is_unit(i - 2):
                     planes_of[i - 2] = first_layer_tanh(i - 2, accs1_of[i - 2])
+                if i == 2:
+                    regroup_second_weight(2, nc.scalar.copy, slice(0, 256))
+                if i == 3:
+                    regroup_second_weight(2, nc.scalar.copy, slice(256, 512))
+                if i == 4:
+                    regroup_second_weight(3, nc.scalar.copy, slice(0, 256))
                 if is_unit(i - 5):
                     accs2_of[i - 5] = second_layer_matmuls(i - 5)
                 if 2 <= i < N_UNITS:

@@ -34,7 +34,6 @@ def tile_rvnn_pa_t_kernel(
         x_pool = ctx.enter_context(tc.tile_pool(name="x_pool", bufs=N_UNITS))
         work = ctx.enter_context(tc.tile_pool(name="work", bufs=3))
         codes_pool = ctx.enter_context(tc.tile_pool(name="codes_pool", bufs=4))
-        out_pool = ctx.enter_context(tc.tile_pool(name="out_pool", bufs=4))
         psum_1 = ctx.enter_context(tc.psum_pool(name="psum_1", bufs=4))
         psum_2 = ctx.enter_context(tc.psum_pool(name="psum_2", bufs=4))
 
@@ -236,7 +235,7 @@ def tile_rvnn_pa_t_kernel(
             return accs
 
         def add_bias(accs):
-            total = out_pool.tile([P, 2, WIDTH], F32, tag="total")
+            total = x_pool.tile([P, 2, WIDTH], F32, tag="x", name="total")
             for k in range(2):
                 nc.vector.tensor_tensor(out=total[:, k, :], in0=accs[k][:], in1=bl_all[:], op=ALU.add)
             return total
@@ -279,8 +278,8 @@ def tile_rvnn_pa_t_kernel(
 
         def gpsimd_cols(u):
             if u < 3:
-                return 320
-            return 448 if u < 14 else 192
+                return 384
+            return 512 if u < 14 else 192
 
         E1_ON_VECTOR = (0,)
         banks_of = {}
@@ -344,14 +343,14 @@ def tile_rvnn_pa_t_kernel(
                     w_q[2] = quantise(flat(w_grouped[2]), "w")
                 if i == 5:
                     w_q[3] = quantise(flat(w_grouped[3]), "w")
-                if is_unit(i + 1):
-                    orient(i + 1)
                 if is_unit(i - 3) and g_cols < BLOCK:
                     regroup(nc.vector.tensor_copy, i - 3, slice(g_cols, BLOCK))
-                if is_unit(i - 1):
-                    h_q[i - 1] = quantise(ht[:], "h")
+                if is_unit(i + 1):
+                    orient(i + 1)
                 if is_unit(i - 3):
                     z_q[i - 3] = quantise(flat(grouped_of[i - 3]), "z", bufs=8)
+                if is_unit(i - 1):
+                    h_q[i - 1] = quantise(ht[:], "h")
                 if is_unit(i - 2):
                     planes_of[i - 2] = first_layer_tanh(i - 2, accs1_of[i - 2])
                 if i == 2:

@@ -281,7 +281,7 @@ def tile_rvnn_pa_t_kernel(
                 return 384
             return 512 if u < 14 else 192
 
-        E1_ON_VECTOR = (0,)
+        E1_ON_VECTOR = (0, 1,)
         banks_of = {}
         h_q = {}
         accs1_of = {}
@@ -296,14 +296,15 @@ def tile_rvnn_pa_t_kernel(
             orient(0)
             banks_of[0] = transpose_unit(0)
             regroup_first_weight(0, nc.scalar.copy, 0, 3)
+            regroup_first_weight(1, nc.scalar.copy, 0, 4)
             regroup_first_weight(0, gpsimd_copy, 3, 4)
             y_v = scaled_on_vector(0, banks_of[0][0])
-            orient(1)
-            banks_of[1] = transpose_unit(1)
             y_s = scaled_on_vector(0, banks_of[0][1])
             ht = new_ht()
             larger(ht, 0, banks_of[0][0], y_v)
             larger(ht, 1, banks_of[0][1], y_s)
+            orient(1)
+            banks_of[1] = transpose_unit(1)
             w_q[0] = quantise(flat(w_grouped[0]), "w")
             h_q[0] = quantise(ht[:], "h")
             for s in range(2):
@@ -312,14 +313,12 @@ def tile_rvnn_pa_t_kernel(
             for i in range(2, N_UNITS + 2):
                 if is_unit(i - 2):
                     accs1_of[i - 2] = first_layer_matmuls(i - 2, h_q[i - 2])
-                if i == 2:
-                    regroup_first_weight(1, gpsimd_copy, 2, 4)
                 if is_unit(i - 3):
                     grouped_of[i - 3] = new_grouped()
                     g_cols = gpsimd_cols(i - 3)
                     for c in range(0, g_cols, g_cols // 1):
                         gpsimd_regroup(i - 3, slice(c, c + g_cols // 1))
-                if is_unit(i - 7):
+                if is_unit(i - 7) and i - 2 < last:
                     finish(i - 7, sums_of[i - 7])
                 if is_unit(i - 1) and i - 1 not in E1_ON_VECTOR:
                     y_s = scaled_on_scalar(i - 1, banks_of[i - 1][1])
@@ -333,8 +332,6 @@ def tile_rvnn_pa_t_kernel(
                     ht = new_ht()
                     larger(ht, 0, banks_of[i - 1][0], y_v)
                     larger(ht, 1, banks_of[i - 1][1], y_s)
-                if i == 2:
-                    regroup_first_weight(1, nc.vector.tensor_copy, 0, 2)
                 if i == 4:
                     regroup_second_weight(3, nc.vector.tensor_copy, slice(256, 512))
                 if i == 2:
@@ -353,6 +350,8 @@ def tile_rvnn_pa_t_kernel(
                     h_q[i - 1] = quantise(ht[:], "h")
                 if is_unit(i - 2):
                     planes_of[i - 2] = first_layer_tanh(i - 2, accs1_of[i - 2])
+                if i - 2 == last:
+                    finish(i - 7, sums_of[i - 7])
                 if i == 2:
                     regroup_second_weight(2, nc.scalar.copy, slice(0, 256))
                 if i == 3:
@@ -383,7 +382,7 @@ def tile_rvnn_pa_t_kernel(
                 )
 
             regroup(nc.vector.tensor_copy, last, slice(0, 256))
-            regroup(nc.vector.tensor_copy, last, slice(256, 384))
+            regroup(nc.scalar.copy, last, slice(256, 384))
             quantise_last(slice(0, 256))
             quantise_last(slice(256, 512))
             sums_of[last - 2] = add_bias(accs2_of[last - 2])

@@ -117,9 +117,18 @@ def tile_rvnn_pa_t_kernel(
             for n in range(4)
         ]
 
-        def regroup_first_weight(n, copy, t0, t1):
+        def scalar_signed(n, out, in_):
+            nc.scalar.activation(out=out, in_=in_, func=ACT.Copy, scale=signs[n][:, 0:1])
+
+        def gpsimd_signed(n, out, in_):
+            nc.gpsimd.tensor_scalar(
+                out=out, in0=in_, scalar1=signs[n][:, 0:1], scalar2=0.0, op0=ALU.mult, op1=ALU.add
+            )
+
+        def regroup_first_weight(n, signed, t0, t1):
             for t in range(t0, t1):
-                copy(
+                signed(
+                    n,
                     out=w_grouped[n][:, t * P : (t + 1) * P, :],
                     in_=(wc_raw, wp_raw)[n][:].rearrange("p j (q t) -> p t q j", t=PACK)[:, t, :, :],
                 )
@@ -207,11 +216,11 @@ def tile_rvnn_pa_t_kernel(
             return accs
 
         def first_layer_tanh(u, accs):
-            planes = work.tile([P, PACK, BLOCK], BF16, tag="planes", bufs=4)
+            planes = x_tiles[u]
             for t in range(PACK):
                 nc.scalar.activation(
                     out=planes[:, t, :], in_=accs[t][:], func=ACT.Tanh,
-                    bias=biases[u % 2][:, t : t + 1], scale=signs[u % 2][:, 0:1],
+                    bias=biases[u % 2][:, t : t + 1], scale=1.0,
                 )
             return planes
 
@@ -234,8 +243,9 @@ def tile_rvnn_pa_t_kernel(
                 accs.append(acc)
             return accs
 
-        def add_bias(accs):
-            total = x_pool.tile([P, 2, WIDTH], F32, tag="x", name="total")
+        def add_bias(n, accs):
+            total = x_tiles[n][:].rearrange("p a k -> p (a k)").bitcast(F32)
+            total = total.rearrange("p (k c) -> p k c", k=2)
             for k in range(2):
                 nc.vector.tensor_tensor(out=total[:, k, :], in0=accs[k][:], in1=bl_all[:], op=ALU.add)
             return total
@@ -281,7 +291,7 @@ def tile_rvnn_pa_t_kernel(
                 return 384
             return 512 if u < 14 else 192
 
-        E1_ON_VECTOR = (0, 1,)
+        E1_ON_VECTOR = (0, 1, 2, 3,)
         banks_of = {}
         h_q = {}
         accs1_of = {}
@@ -295,9 +305,8 @@ def tile_rvnn_pa_t_kernel(
         with tc.manual_schedule():
             orient(0)
             banks_of[0] = transpose_unit(0)
-            regroup_first_weight(0, nc.scalar.copy, 0, 3)
-            regroup_first_weight(1, nc.scalar.copy, 0, 4)
-            regroup_first_weight(0, gpsimd_copy, 3, 4)
+            regroup_first_weight(0, scalar_signed, 0, 4)
+            regroup_first_weight(1, scalar_signed, 0, 4)
             y_v = scaled_on_vector(0, banks_of[0][0])
             y_s = scaled_on_vector(0, banks_of[0][1])
             ht = new_ht()
@@ -327,16 +336,14 @@ def tile_rvnn_pa_t_kernel(
                     if i - 1 in E1_ON_VECTOR:
                         y_s = scaled_on_vector(i - 1, banks_of[i - 1][1])
                 if is_unit(i - 6):
-                    sums_of[i - 6] = add_bias(accs2_of[i - 6])
+                    sums_of[i - 6] = add_bias(i - 6, accs2_of[i - 6])
                 if is_unit(i - 1):
                     ht = new_ht()
                     larger(ht, 0, banks_of[i - 1][0], y_v)
                     larger(ht, 1, banks_of[i - 1][1], y_s)
-                if i == 4:
-                    regroup_second_weight(3, nc.vector.tensor_copy, slice(256, 512))
                 if i == 2:
                     w_q[1] = quantise(flat(w_grouped[1]), "w")
-                if i == 4:
+                if i == 3:
                     w_q[2] = quantise(flat(w_grouped[2]), "w")
                 if i == 5:
                     w_q[3] = quantise(flat(w_grouped[3]), "w")
@@ -353,18 +360,18 @@ def tile_rvnn_pa_t_kernel(
                 if i - 2 == last:
                     finish(i - 7, sums_of[i - 7])
                 if i == 2:
-                    regroup_second_weight(2, nc.scalar.copy, slice(0, 256))
+                    regroup_second_weight(2, nc.scalar.copy, slice(0, 512))
                 if i == 3:
-                    regroup_second_weight(2, nc.scalar.copy, slice(256, 512))
-                if i == 4:
                     regroup_second_weight(3, nc.scalar.copy, slice(0, 256))
+                if i == 4:
+                    regroup_second_weight(3, nc.scalar.copy, slice(256, 512))
                 if is_unit(i - 5):
                     accs2_of[i - 5] = second_layer_matmuls(i - 5)
                 if 2 <= i < N_UNITS:
                     banks_of[i] = transpose_unit(i)
 
             accs2_of[last - 2] = second_layer_matmuls(last - 2)
-            sums_of[last - 3] = add_bias(accs2_of[last - 3])
+            sums_of[last - 3] = add_bias(last - 3, accs2_of[last - 3])
             grouped_of[last] = new_grouped()
             gpsimd_regroup(last, slice(384, 512))
             codes = codes_pool.tile(
@@ -385,10 +392,10 @@ def tile_rvnn_pa_t_kernel(
             regroup(nc.scalar.copy, last, slice(256, 384))
             quantise_last(slice(0, 256))
             quantise_last(slice(256, 512))
-            sums_of[last - 2] = add_bias(accs2_of[last - 2])
+            sums_of[last - 2] = add_bias(last - 2, accs2_of[last - 2])
             for n in range(last - 4, last - 1):
                 finish(n, sums_of[n])
             for n in (last - 1, last):
                 accs2_of[n] = second_layer_matmuls(n)
-                sums_of[n] = add_bias(accs2_of[n])
+                sums_of[n] = add_bias(n, accs2_of[n])
                 finish(n, sums_of[n])

@@ -271,9 +271,7 @@ def tile_rvnn_pa_t_kernel(
             )
 
         def gpsimd_regroup(u, cols):
-            gpsimd_copy(
-                out=grouped_of[u][:, cols, :], in_=planes_of[u][:, :, cols].rearrange("p t c -> p c t")
-            )
+            regroup(gpsimd_copy, u, cols)
 
         def new_grouped():
             return work.tile(

from contextlib import ExitStack

import concourse.mybir as mybir
from concourse.masks import make_identity

F32 = mybir.dt.float32
BF16 = mybir.dt.bfloat16
U32 = mybir.dt.uint32
U8 = mybir.dt.uint8
FP8X4 = mybir.dt.float8_e4m3fn_x4
ALU = mybir.AluOpType
ACT = mybir.ActivationFunctionType

P = 128
PACK = 4
ROWS = 4096
WIDTH = 512
BLOCK = 512
ROW_TILES = BLOCK // P
N_BLOCKS = ROWS // BLOCK
N_UNITS = 2 * N_BLOCKS

FLOPS = 2 * ROWS * WIDTH * WIDTH * 2 + 2 * ROWS * (2 * WIDTH) * WIDTH


def tile_rvnn_pa_t_kernel(
    tc, pre_child, pre_parent, ac, Wc2, bc2, ap, Wp2, bp2, Wl1, bl1, out
):
    nc = tc.nc
    streams = (pre_child, pre_parent)

    with ExitStack() as ctx:
        const = ctx.enter_context(tc.tile_pool(name="const", bufs=1))
        x_pool = ctx.enter_context(tc.tile_pool(name="x_pool", bufs=N_UNITS))
        work = ctx.enter_context(tc.tile_pool(name="work", bufs=3))
        codes_pool = ctx.enter_context(tc.tile_pool(name="codes_pool", bufs=4))
        psum_1 = ctx.enter_context(tc.psum_pool(name="psum_1", bufs=4))
        psum_2 = ctx.enter_context(tc.psum_pool(name="psum_2", bufs=4))

        first_halves = (slice(0, 2), slice(2, 4))

        def load_x(u):
            b, s = divmod(u, 2)
            x = x_pool.tile([P, ROW_TILES, WIDTH], BF16, tag="x", name="x%d" % u)
            rows = streams[s][b * BLOCK : (b + 1) * BLOCK, :]
            rows = rows.rearrange("(p a) k -> p a k", a=ROW_TILES)
            for part in first_halves if u == 0 else (slice(0, ROW_TILES),):
                nc.sync.dma_start(out=x[:, part, :], in_=rows[:, part, :])
            return x

        def load_first_weight(w, name):
            raw = const.tile([P, PACK, WIDTH], BF16, name=name)
            nc.sync.dma_start(
                out=raw[:].rearrange("p (h e) c -> p h e c", e=2),
                in_=w.rearrange("(h p e) c -> p h e c", h=2, e=2),
            )
            return raw

        slopes_bf = []
        with nc.allow_non_contiguous_dma(reason="a few small vectors, once"):
            for s, a_in in enumerate((ac, ap)):
                a_bf = const.tile([P, 1], BF16, name="a_bf%d" % s)
                nc.sync.dma_start(out=a_bf[:], in_=a_in.partition_broadcast(P))
                slopes_bf.append(a_bf)
        x_tiles = [load_x(0)]
        wc_raw = load_first_weight(Wc2, "wc_raw")
        x_tiles.append(load_x(1))
        wp_raw = load_first_weight(Wp2, "wp_raw")
        x_tiles.append(load_x(2))
        wl_raw = const.tile([P, 2, PACK, WIDTH], BF16, name="wl_raw")
        nc.sync.dma_start(out=wl_raw[:], in_=Wl1.rearrange("(g p j) c -> p g j c", g=2, j=PACK))
        for u in range(3, 8):
            x_tiles.append(load_x(u))
        bl_all = const.tile([P, WIDTH], BF16, name="bl_all")
        with nc.allow_non_contiguous_dma(reason="one small vector, once"):
            nc.sync.dma_start(out=bl_all[:], in_=bl1.partition_broadcast(P))
        for u in range(8, N_UNITS):
            x_tiles.append(load_x(u))

        biases_bf = []
        with nc.allow_non_contiguous_dma(reason="a few small vectors, once"):
            for s, b_in in enumerate((bc2, bp2)):
                b_bf = const.tile([P, PACK], BF16, name="b_bf%d" % s)
                nc.scalar.dma_start(out=b_bf[:], in_=b_in.rearrange("(p t) -> p t", t=PACK))
                biases_bf.append(b_bf)

        warm = const.tile([P, 1], F32, name="warm")
        nc.vector.memset(warm[:], 0.0)
        nc.scalar.activation(out=warm[:], in_=warm[:], func=ACT.Tanh)

        above = [const.tile([P, 1], F32, name="above%d" % s) for s in range(2)]
        signs = [const.tile([P, 1], F32, name="sign%d" % s) for s in range(2)]
        slopes = [const.tile([P, 1], F32, name="a_f%d" % s) for s in range(2)]
        biases = [const.tile([P, PACK], F32, name="b_f%d" % s) for s in range(2)]
        for s in range(2):
            nc.vector.tensor_scalar(
                out=above[s][:], in0=slopes_bf[s][:], scalar1=1.0, scalar2=-2.0,
                op0=ALU.is_gt, op1=ALU.mult,
            )
        for s in range(2):
            nc.vector.tensor_scalar(
                out=signs[s][:], in0=above[s][:], scalar1=1.0, scalar2=None, op0=ALU.add
            )
        for s in range(2):
            nc.vector.tensor_copy(out=slopes[s][:], in_=slopes_bf[s][:])

        ident = const.tile([P, P], F32, name="ident")
        make_identity(nc, ident[:])

        def gpsimd_copy(out, in_):
            nc.gpsimd.tensor_scalar(
                out=out, in0=in_, scalar1=1.0, scalar2=0.0, op0=ALU.mult, op1=ALU.add
            )

        w_grouped = [
            const.tile([P, WIDTH, PACK], BF16, name="w_grouped%d" % n, align_bytes=64)
            for n in range(4)
        ]

        def scalar_signed(n, out, in_):
            nc.scalar.activation(out=out, in_=in_, func=ACT.Copy, scale=signs[n][:, 0:1])

        def gpsimd_signed(n, out, in_):
            nc.gpsimd.tensor_scalar(
                out=out, in0=in_, scalar1=signs[n][:, 0:1], scalar2=0.0, op0=ALU.mult, op1=ALU.add
            )

        def regroup_first_weight(n, signed, t0, t1):
            for t in range(t0, t1):
                signed(
                    n,
                    out=w_grouped[n][:, t * P : (t + 1) * P, :],
                    in_=(wc_raw, wp_raw)[n][:].rearrange("p j (q t) -> p t q j", t=PACK)[:, t, :, :],
                )

        def regroup_second_weight(n, copy, cols):
            copy(
                out=w_grouped[n][:, cols, :].rearrange("p (c i) j -> p c j i", i=4),
                in_=wl_raw[:, n - 2, :, cols].rearrange("p j (c i) -> p c j i", i=4),
            )

        def quantise(values, tag, bufs=4):
            codes = codes_pool.tile([P, BLOCK], U32, tag=tag + "_codes", bufs=bufs, align_bytes=64)
            scales = codes_pool.tile([P, BLOCK], U8, tag=tag + "_scales", bufs=bufs, align_bytes=64)
            nc.vector.quantize_mx(out=codes[:].bitcast(FP8X4), scales=scales[:], in_=values)
            return codes, scales

        def orient(u):
            for part in first_halves if u == 0 else (slice(0, ROW_TILES),):
                x = x_tiles[u][:, part, :]
                nc.vector.tensor_scalar(
                    out=x, in0=x, scalar1=signs[u % 2][:, 0:1], scalar2=None, op0=ALU.mult
                )

        def transpose_unit(u):
            words = x_tiles[u][:].rearrange("p a k -> p (a k)").bitcast(F32)
            words = words.rearrange("p (a w) -> p a w", a=ROW_TILES)
            banks = []
            for half in range(2):
                bank = psum_2.tile([P, 2, 2 * P], F32, tag="bank")
                for a in range(2):
                    for h in range(2):
                        nc.tensor.transpose(
                            bank[:, h, a * P : (a + 1) * P],
                            words[:, 2 * half + a, h * P : (h + 1) * P],
                            ident[:],
                        )
                banks.append(bank)
            return banks

        def bank_values(bank):
            flat = bank[:].rearrange("p h q -> p (h q)").bitcast(BF16)
            return flat.rearrange("p (h q e) -> p q h e", h=2, e=2)

        def as_rows(flat):
            return flat.rearrange("p (q h e) -> p q h e", h=2, e=2)

        def scaled_on_vector(u, bank):
            y = work.tile([P, 2 * WIDTH], BF16, tag="yv")
            nc.vector.tensor_scalar(
                out=as_rows(y[:]), in0=bank_values(bank), scalar1=slopes[u % 2][:, 0:1],
                scalar2=None, op0=ALU.mult,
            )
            return y

        def scaled_on_scalar(u, bank):
            y = work.tile([P, 2 * WIDTH], BF16, tag="ys")
            nc.scalar.activation(
                out=as_rows(y[:]), in_=bank_values(bank), func=ACT.Copy,
                scale=slopes[u % 2][:, 0:1],
            )
            return y

        def larger(ht, half, bank, y):
            nc.vector.tensor_tensor(
                out=as_rows(ht[:, half * 1024 : (half + 1) * 1024]),
                in0=bank_values(bank), in1=as_rows(y[:]), op=ALU.max,
            )

        def first_layer_matmuls(u, h):
            s = u % 2
            accs = []
            for t in range(PACK):
                acc = psum_1.tile([P, BLOCK], F32, tag="acc1")
                cols = slice(t * P, (t + 1) * P)
                nc.tensor.matmul_mx(
                    out=acc[:],
                    lhsT=w_q[s][0][:, cols].bitcast(FP8X4),
                    lhsT_scale=w_q[s][1][:, cols],
                    rhs=h[0][:].bitcast(FP8X4),
                    rhs_scale=h[1][:],
                    start=True,
                    stop=True,
                )
                accs.append(acc)
            return accs

        def first_layer_tanh(u, accs):
            planes = x_tiles[u]
            for t in range(PACK):
                nc.scalar.activation(
                    out=planes[:, t, :], in_=accs[t][:], func=ACT.Tanh,
                    bias=biases[u % 2][:, t : t + 1], scale=1.0,
                )
            return planes

        def second_layer_matmuls(n):
            b, half = divmod(n, 2)
            accs = []
            for a in (2 * half, 2 * half + 1):
                acc = psum_2.tile([P, WIDTH], F32, tag="bank")
                cols = slice(a * P, (a + 1) * P)
                for g in range(2):
                    nc.tensor.matmul_mx(
                        out=acc[:],
                        lhsT=z_q[2 * b + g][0][:, cols].bitcast(FP8X4),
                        lhsT_scale=z_q[2 * b + g][1][:, cols],
                        rhs=w_q[2 + g][0][:].bitcast(FP8X4),
                        rhs_scale=w_q[2 + g][1][:],
                        start=(g == 0),
                        stop=(g == 1),
                    )
                accs.append(acc)
            return accs

        def add_bias(n, accs):
            total = x_tiles[n][:].rearrange("p a k -> p (a k)").bitcast(F32)
            total = total.rearrange("p (k c) -> p k c", k=2)
            for k in range(2):
                nc.vector.tensor_tensor(out=total[:, k, :], in0=accs[k][:], in1=bl_all[:], op=ALU.add)
            return total

        def finish(n, total):
            b, half = divmod(n, 2)
            rows = out[b * BLOCK : (b + 1) * BLOCK, :].rearrange("(p a) c -> p a c", a=ROW_TILES)
            pieces = (slice(0, 1), slice(1, 2)) if n == N_UNITS - 1 else (slice(0, 2),)
            for part in pieces:
                nc.scalar.activation(out=total[:, part, :], in_=total[:, part, :], func=ACT.Tanh)
                nc.sync.dma_start(
                    out=rows[:, 2 * half + part.start : 2 * half + part.stop, :],
                    in_=total[:, part, :],
                )

        def is_unit(u):
            return 0 <= u < N_UNITS

        def regroup(copy, u, cols):
            copy(
                out=grouped_of[u][:, cols, :].rearrange("p (c i) t -> p c t i", i=4),
                in_=planes_of[u][:, :, cols].rearrange("p t (c i) -> p c t i", i=4),
            )

        def gpsimd_regroup(u, cols):
            regroup(gpsimd_copy, u, cols)

        def new_grouped():
            return work.tile(
                [P, BLOCK, PACK], BF16, tag="z_grouped", name="z_grouped", bufs=1, align_bytes=64
            )

        def flat(grouped):
            return grouped[:].rearrange("p c t -> p (c t)")

        def new_ht():
            return work.tile([P, BLOCK * PACK], BF16, tag="ht", name="ht", align_bytes=64)

        def gpsimd_cols(u):
            if u < 3:
                return 384
            return 512 if u < 14 else 192

        E1_ON_VECTOR = (0, 1, 2, 3,)
        banks_of = {}
        h_q = {}
        accs1_of = {}
        planes_of = {}
        grouped_of = {}
        z_q = {}
        accs2_of = {}
        sums_of = {}
        w_q = {}
        last = N_UNITS - 1
        with tc.manual_schedule():
            orient(0)
            banks_of[0] = transpose_unit(0)
            regroup_first_weight(0, scalar_signed, 0, 4)
            regroup_first_weight(1, scalar_signed, 0, 4)
            y_v = scaled_on_vector(0, banks_of[0][0])
            y_s = scaled_on_vector(0, banks_of[0][1])
            ht = new_ht()
            larger(ht, 0, banks_of[0][0], y_v)
            larger(ht, 1, banks_of[0][1], y_s)
            orient(1)
            banks_of[1] = transpose_unit(1)
            w_q[0] = quantise(flat(w_grouped[0]), "w")
            h_q[0] = quantise(ht[:], "h")
            for s in range(2):
                nc.vector.tensor_copy(out=biases[s][:], in_=biases_bf[s][:])
            orient(2)
            for i in range(2, N_UNITS + 2):
                if is_unit(i - 2):
                    accs1_of[i - 2] = first_layer_matmuls(i - 2, h_q[i - 2])
                if is_unit(i - 3):
                    grouped_of[i - 3] = new_grouped()
                    g_cols = gpsimd_cols(i - 3)
                    for c in range(0, g_cols, g_cols // 1):
                        gpsimd_regroup(i - 3, slice(c, c + g_cols // 1))
                if is_unit(i - 7) and i - 2 < last:
                    finish(i - 7, sums_of[i - 7])
                if is_unit(i - 1) and i - 1 not in E1_ON_VECTOR:
                    y_s = scaled_on_scalar(i - 1, banks_of[i - 1][1])
                if is_unit(i - 1):
                    y_v = scaled_on_vector(i - 1, banks_of[i - 1][0])
                    if i - 1 in E1_ON_VECTOR:
                        y_s = scaled_on_vector(i - 1, banks_of[i - 1][1])
                if is_unit(i - 6):
                    sums_of[i - 6] = add_bias(i - 6, accs2_of[i - 6])
                if is_unit(i - 1):
                    ht = new_ht()
                    larger(ht, 0, banks_of[i - 1][0], y_v)
                    larger(ht, 1, banks_of[i - 1][1], y_s)
                if i == 2:
                    w_q[1] = quantise(flat(w_grouped[1]), "w")
                if i == 3:
                    w_q[2] = quantise(flat(w_grouped[2]), "w")
                if i == 5:
                    w_q[3] = quantise(flat(w_grouped[3]), "w")
                if is_unit(i - 3) and g_cols < BLOCK:
                    regroup(nc.vector.tensor_copy, i - 3, slice(g_cols, BLOCK))
                if is_unit(i + 1):
                    orient(i + 1)
                if is_unit(i - 3):
                    z_q[i - 3] = quantise(flat(grouped_of[i - 3]), "z", bufs=8)
                if is_unit(i - 1):
                    h_q[i - 1] = quantise(ht[:], "h")
                if is_unit(i - 2):
                    planes_of[i - 2] = first_layer_tanh(i - 2, accs1_of[i - 2])
                if i - 2 == last:
                    finish(i - 7, sums_of[i - 7])
                if i == 2:
                    regroup_second_weight(2, nc.scalar.copy, slice(0, 512))
                if i == 3:
                    regroup_second_weight(3, nc.scalar.copy, slice(0, 256))
                if i == 4:
                    regroup_second_weight(3, nc.scalar.copy, slice(256, 512))
                if is_unit(i - 5):
                    accs2_of[i - 5] = second_layer_matmuls(i - 5)
                if 2 <= i < N_UNITS:
                    banks_of[i] = transpose_unit(i)

            accs2_of[last - 2] = second_layer_matmuls(last - 2)
            sums_of[last - 3] = add_bias(last - 3, accs2_of[last - 3])
            grouped_of[last] = new_grouped()
            gpsimd_regroup(last, slice(384, 512))
            codes = codes_pool.tile(
                [P, BLOCK], U32, tag="z_codes", name="last_codes", bufs=8, align_bytes=64
            )
            scales = codes_pool.tile(
                [P, BLOCK], U8, tag="z_scales", name="last_scales", bufs=8, align_bytes=64
            )
            z_q[last] = (codes, scales)

            def quantise_last(cols):
                nc.vector.quantize_mx(
                    out=codes[:, cols].bitcast(FP8X4), scales=scales[:, cols],
                    in_=grouped_of[last][:, cols, :].rearrange("p c t -> p (c t)"),
                )

            regroup(nc.vector.tensor_copy, last, slice(0, 256))
            regroup(nc.scalar.copy, last, slice(256, 384))
            quantise_last(slice(0, 256))
            quantise_last(slice(256, 512))
            sums_of[last - 2] = add_bias(last - 2, accs2_of[last - 2])
            for n in range(last - 4, last - 1):
                finish(n, sums_of[n])
            for n in (last - 1, last):
                accs2_of[n] = second_layer_matmuls(n)
                sums_of[n] = add_bias(n, accs2_of[n])
                finish(n, sums_of[n])
